import numpy as np
import ml_dtypes


def mxq(x, axis, fmt="e4m3"):
    dtype, down = {"e4m3": (ml_dtypes.float8_e4m3fn, 7), "e5m2": (ml_dtypes.float8_e5m2, 14)}[fmt]
    v = np.moveaxis(np.asarray(x, np.float32).astype(ml_dtypes.bfloat16).astype(np.float64), axis, -1)
    blocks = v.reshape(v.shape[:-1] + (-1, 32))
    amax = np.abs(blocks).max(-1, keepdims=True)
    byte = np.maximum(np.where(amax > 0, np.frexp(amax)[1] - 1 + 127, 0) - down, 1)
    scale = np.exp2(byte - 127.0)
    codes = (blocks / scale).astype(np.float32).astype(dtype).astype(np.float64)
    return np.moveaxis((codes * scale).reshape(v.shape), -1, axis)


WIDE = False


def mx_kscale(k):
    if not WIDE:
        return np.ones(k)
    levels = np.array([20, -20, 10, -10, 0])
    a = np.random.permutation(np.resize(levels, k // 512 * 4)).reshape(k // 512, 4)
    idx = np.arange(k)
    return np.exp2(a[idx // 512, idx % 128 // 32])


BF16 = ml_dtypes.bfloat16


def bf(x):
    return np.asarray(x, np.float32).astype(BF16)


def f64(x):
    return np.asarray(x).astype(np.float64)


B, N, D = 2, 2048, 512
LAMBDA_RG = 64.0


def setup_inputs():
    u = mx_kscale(D)
    latent = np.random.standard_normal((B, N, D)) / u
    alpha = np.random.uniform(0.0, 1.0, (B, N))
    g = np.random.standard_normal((B, N, D)) * np.exp2(np.random.randint(-12, 1, (B, N, 1))) * u
    return {"latent": bf(latent), "alpha": bf(alpha), "grad_out": bf(g)}


def reference(latent, alpha, grad_out):
    latent, alpha, g = f64(latent), f64(alpha), f64(grad_out)
    n = latent.shape[1]
    idx = np.arange(n)
    r = np.abs(idx[:, None] - idx[None, :]).astype(np.float64) + 1e-4
    alpha_pair = (alpha[:, :, None] + alpha[:, None, :]) * 0.5
    k = np.power(r[None], -alpha_pair) * np.exp(-r / LAMBDA_RG)[None]
    kn = k / (np.sum(k, axis=-1, keepdims=True) + 1e-8)
    p = mxq(g, 2, "e5m2") @ mxq(latent, 2, "e4m3").transpose(0, 2, 1)
    c = np.sum(p * kn, axis=2, keepdims=True)
    da = -(p - c) * kn * np.log(r)[None]
    return 0.5 * (np.sum(da, axis=2) + np.sum(da, axis=1))

@@ -1,0 +1,409 @@
+from contextlib import ExitStack
+
+import concourse.mybir as mybir
+from concourse.masks import make_identity
+
+F32 = mybir.dt.float32
+BF16 = mybir.dt.bfloat16
+U32 = mybir.dt.uint32
+U8 = mybir.dt.uint8
+I32 = mybir.dt.int32
+E4X4 = mybir.dt.float8_e4m3fn_x4
+E5X4 = mybir.dt.float8_e5m2_x4
+ACT = mybir.ActivationFunctionType
+ALU = mybir.AluOpType
+AX = mybir.AxisListType
+
+P = 128
+B = 2
+N = 2048
+D = 512
+NT = N // P
+CH = 512
+NC = N // CH
+EPS = 1e-4
+LAM = 64.0
+CEN = N - P
+TABW = 2 * N - P
+STEPS = B * NT
+
+FLOPS = 2 * B * N * N * D
+
+
+def tile_csocrgattention_kernel(tc, latent, alpha, grad_out, out):
+    nc = tc.nc
+    with ExitStack() as ctx:
+        const = ctx.enter_context(tc.tile_pool(name="const", bufs=1))
+        codes = ctx.enter_context(tc.tile_pool(name="codes", bufs=1))
+        stage = ctx.enter_context(tc.tile_pool(name="stage", bufs=2))
+        kpool = ctx.enter_context(tc.tile_pool(name="kpool", bufs=1))
+        upool = ctx.enter_context(tc.tile_pool(name="upool", bufs=2))
+        work = ctx.enter_context(tc.tile_pool(name="work", bufs=3))
+        small = ctx.enter_context(tc.tile_pool(name="small", bufs=3))
+        psp = ctx.enter_context(tc.psum_pool(name="psp", bufs=4))
+        pst = ctx.enter_context(tc.psum_pool(name="pst", bufs=3))
+        psc = ctx.enter_context(tc.psum_pool(name="psc", bufs=1))
+        ctx.enter_context(tc.manual_schedule())
+
+        ident = const.tile([P, P], F32)
+        make_identity(nc, ident[:])
+        d0i = const.tile([P, P], I32)
+        nc.gpsimd.iota(d0i[:], pattern=[[-1, P]], base=0, channel_multiplier=1)
+        rowi = const.tile([P, NT], I32)
+        nc.gpsimd.iota(rowi[:], pattern=[[P, NT]], base=-(N // 2), channel_multiplier=1)
+
+        abf = const.tile([P, P], BF16)
+        nc.vector.memset(abf[:], 0.0)
+        nc.sync.dma_start(out=abf[0 : B * NT, :], in_=alpha.rearrange("b (t p) -> (b t) p", p=P))
+
+        d0 = const.tile([P, P], F32)
+        nc.vector.tensor_copy(out=d0[:], in_=d0i[:])
+        nd0 = const.tile([P, P], F32)
+        nc.vector.tensor_scalar(out=nd0[:], in0=d0[:], scalar1=-1.0, scalar2=None, op0=ALU.mult)
+        rd = const.tile([P, P], F32)
+        nc.vector.tensor_tensor(out=rd[:], in0=d0[:], in1=nd0[:], op=ALU.max)
+        nc.vector.tensor_scalar(out=rd[:], in0=rd[:], scalar1=EPS, scalar2=None, op0=ALU.add)
+
+        tab = const.tile([P, TABW], F32)
+        nc.vector.tensor_scalar(out=tab[:, CEN - P : CEN], in0=d0[:], scalar1=P + EPS, scalar2=None, op0=ALU.add)
+        filled = P
+        while filled < CEN:
+            n = min(filled, CEN - filled)
+            nc.vector.tensor_scalar(
+                out=tab[:, CEN - filled - n : CEN - filled], in0=tab[:, CEN - n : CEN],
+                scalar1=float(filled), scalar2=None, op0=ALU.add,
+            )
+            filled += n
+        R0 = CEN + P
+        nc.vector.tensor_scalar(out=tab[:, R0 : R0 + P], in0=nd0[:], scalar1=P + EPS, scalar2=None, op0=ALU.add)
+        filled = P
+        while filled < CEN:
+            n = min(filled, CEN - filled)
+            nc.vector.tensor_scalar(
+                out=tab[:, R0 + filled : R0 + filled + n], in0=tab[:, R0 : R0 + n],
+                scalar1=float(filled), scalar2=None, op0=ALU.add,
+            )
+            filled += n
+        nc.scalar.activation(out=tab[:, CEN:R0], in_=rd[:], func=ACT.Ln)
+        nc.scalar.activation(out=tab[:, 0:CEN], in_=tab[:, 0:CEN], func=ACT.Ln)
+        nc.scalar.activation(out=tab[:, R0:TABW], in_=tab[:, R0:TABW], func=ACT.Ln)
+        sqt = const.tile([P, P], F32)
+        nc.scalar.activation(out=sqt[:], in_=rd[:], func=ACT.Exp, scale=-0.5 / LAM)
+
+        br = const.tile([P, NT], F32)
+        nc.vector.tensor_scalar(out=br[:], in0=rowi[:], scalar1=1.0 / LAM, scalar2=None, op0=ALU.mult)
+        bl = const.tile([P, NT], F32)
+        nc.vector.tensor_scalar(out=bl[:], in0=rowi[:], scalar1=-1.0 / LAM, scalar2=-EPS / LAM, op0=ALU.mult, op1=ALU.add)
+
+        af = const.tile([P, P], F32)
+        nc.vector.tensor_copy(out=af[:], in_=abf[:])
+        aps = pst.tile([P, CH], F32, tag="tp")
+        nc.tensor.transpose(aps[:, 0:P], af[:], ident[:])
+        nega = const.tile([P, STEPS], F32)
+        nc.vector.tensor_scalar(out=nega[:], in0=aps[:, 0:STEPS], scalar1=-0.5, scalar2=None, op0=ALU.mult)
+
+        ws = const.tile([P, STEPS], F32)
+        rpart = const.tile([P, STEPS * NC], F32)
+        cacc = psc.tile([P, CH], F32)
+        junk = const.tile([P, CH], F32)
+
+        gc = [codes.tile([P, N], U32, name="gc%d" % b, align_bytes=64) for b in range(B)]
+        gs = [codes.tile([P, N], U8, name="gs%d" % b, align_bytes=64) for b in range(B)]
+        lc = [codes.tile([P, N], U32, name="lc%d" % b, align_bytes=64) for b in range(B)]
+        ls = [codes.tile([P, N], U8, name="ls%d" % b, align_bytes=64) for b in range(B)]
+
+        groups = [(latent, 0, g, lc[0], ls[0], E4X4) for g in range(4)] + [(grad_out, 0, g, gc[0], gs[0], E5X4) for g in range(4)]
+        groups += [(latent, 1, g, lc[1], ls[1], E4X4) for g in range(4)] + [(grad_out, 1, g, gc[1], gs[1], E5X4) for g in range(4)]
+        HEAD = 5
+        xsbs = {}
+        grps = {}
+
+        def g_load(n):
+            if n < len(groups):
+                src, b, g = groups[n][0:3]
+                xsb = stage.tile([P, 4, D], BF16, tag="xsb", bufs=3)
+                nc.sync.dma_start(out=xsb[:], in_=src[b, CH * g : CH * (g + 1), :].rearrange("(a p) d -> p a d", p=P))
+                xsbs[n] = xsb
+
+        def g_tr(n, on_vector):
+            xsb = xsbs[n]
+            grp = stage.tile([P, 4 * CH], BF16, tag="grp", align_bytes=64)
+            grps[n] = grp
+            gview = grp[:].bitcast(F32).rearrange("p (a r u) -> p a r u", a=4, u=2)
+            for hf in range(2):
+                xt = pst.tile([P, 2, 2, P], F32, tag="tp")
+                for a in range(2):
+                    words = xsb[:, 2 * hf + a, :].bitcast(F32)
+                    for u in range(2):
+                        nc.tensor.transpose(xt[:, a, u, :], words[:, P * u : P * (u + 1)], ident[:])
+                sview = xt[:].rearrange("p a u r -> p a r u")
+                if on_vector:
+                    nc.vector.tensor_copy(out=gview[:, 2 * hf : 2 * hf + 2], in_=sview)
+                else:
+                    nc.scalar.copy(out=gview[:, 2 * hf : 2 * hf + 2], in_=sview)
+
+        def g_q(n):
+            g, cod, pla, fmt = groups[n][2:6]
+            nc.vector.quantize_mx(
+                out=cod[:, CH * g : CH * (g + 1)].bitcast(fmt), scales=pla[:, CH * g : CH * (g + 1)], in_=grps[n][:]
+            )
+
+        kp = {}
+        urows = {}
+        ud0s = {}
+        ulcs = {}
+        kch = {}
+        wch = {}
+        pbs = {}
+        accds = {}
+        accas = {}
+        sigs = {}
+        negcs = {}
+        areds = {}
+        tvs = {}
+
+        def live(t):
+            return 0 <= t < STEPS
+
+        def stage_u(t):
+            if not live(t):
+                return
+            b, i = divmod(t, NT)
+            urow = upool.tile([P, N], F32, tag="urow")
+            ud0 = upool.tile([P, P], F32, tag="ud0")
+            sc = nega[:, t : t + 1]
+            nc.scalar.activation(out=ud0[:], in_=tab[:, CEN:R0], func=ACT.Exp, scale=sc)
+            urows[t] = urow
+            ud0s[t] = ud0
+            if i < NT - 1:
+                ulc = upool.tile([P, N - P], F32, tag="ulc")
+                for j in range(i + 1, NT):
+                    blk = NT - 1 - j + i
+                    nc.scalar.activation(
+                        out=ulc[:, P * (j - i - 1) : P * (j - i)], in_=tab[:, P * blk : P * (blk + 1)], func=ACT.Exp,
+                        scale=nega[:, b * NT + j : b * NT + j + 1], bias=bl[:, j : j + 1],
+                    )
+                ulcs[t] = ulc
+                wd = N - P * (i + 1)
+                nc.scalar.activation(
+                    out=urow[:, P : P + wd], in_=tab[:, R0 : R0 + wd], func=ACT.Exp, scale=sc, bias=br[:, i : i + 1]
+                )
+
+        def pool_ud(t):
+            if live(t):
+                nc.gpsimd.tensor_tensor(out=urows[t][:, 0:P], in0=ud0s[t][:], in1=sqt[:], op=ALU.mult)
+
+        def fill_tv(t, unit):
+            i = t % NT
+            c, lo = unit
+            vt = pst.tile([P, CH], F32, tag="tp")
+            for q in range(lo, 4):
+                j = 4 * c + q
+                if j == i:
+                    srcb = urows[t][:, 0:P]
+                else:
+                    srcb = ulcs[t][:, P * (j - i - 1) : P * (j - i)]
+                nc.tensor.transpose(vt[:, P * (q - lo) : P * (q - lo + 1)], srcb, ident[:])
+            return vt
+
+        def prefetch(t):
+            if not live(t):
+                return
+            b, i = divmod(t, NT)
+            c0, m = divmod(i, 4)
+            kpi = kpool.tile([P, N - CH * c0], F32, tag="kp%d" % i, name="kp%d_%d" % (i, b))
+            kp[i] = kpi
+            accd = small.tile([P, 2 * NC], F32, tag="accd")
+            accds[t] = accd
+            if i > 0:
+                acca = small.tile([P, NC], F32, tag="acca")
+                accas[t] = acca
+            chunks = []
+            for c in range(c0):
+                kt = pst.tile([P, CH], F32, tag="tp")
+                for q in range(4):
+                    j = 4 * c + q
+                    off = P * i - CH * (j // 4)
+                    nc.tensor.transpose(kt[:, P * q : P * (q + 1)], kp[j][:, off : off + P], ident[:])
+                klo = work.tile([P, CH], F32, tag="klo", bufs=6)
+                nc.scalar.activation(out=klo[:], in_=kt[:], func=ACT.Copy, accum_out=acca[:, c : c + 1])
+                chunks.append(klo[:])
+            if m > 0:
+                kt = pst.tile([P, CH], F32, tag="tp")
+                for q in range(m):
+                    nc.tensor.transpose(kt[:, P * q : P * (q + 1)], kp[4 * c0 + q][:, P * m : P * (m + 1)], ident[:])
+                nc.scalar.activation(
+                    out=kpi[:, 0 : P * m], in_=kt[:, 0 : P * m], func=ACT.Copy, accum_out=acca[:, c0 : c0 + 1]
+                )
+            for c in range(c0, NC):
+                chunks.append(kpi[:, CH * (c - c0) : CH * (c - c0 + 1)])
+            kch[t] = chunks
+            units = [(c, m if c == c0 else 0) for c in range(c0, NC)]
+            tvs[t] = [units, [fill_tv(t, un) for un in units[0:3]]]
+
+        def small_a(t):
+            if live(t):
+                ared = small.tile([P, 1], F32, tag="ared")
+                nc.vector.tensor_reduce(out=ared[:], in_=accds[t][:, 0:NC], axis=AX.X, op=ALU.add)
+                areds[t] = ared
+
+        def small_b(t):
+            if live(t):
+                negc = small.tile([P, 1], F32, tag="negc")
+                nc.vector.tensor_scalar(
+                    out=negc[:], in0=areds[t][:], scalar1=sigs[t][:, 0:1], scalar2=-1.0, op0=ALU.mult, op1=ALU.mult
+                )
+                negcs[t] = negc
+
+        def k_phase(t):
+            if not live(t):
+                small_a(t - 1)
+                small_b(t - 1)
+                return
+            i = t % NT
+            c0 = i // 4
+            units, banks = tvs[t]
+            for idx in range(len(units)):
+                c, lo = units[idx]
+                nw = P * (4 - lo)
+                uo = P * (4 * c + lo - i)
+                base = CH * (c - c0)
+                nc.vector.scalar_tensor_tensor(
+                    out=kp[i][:, base + P * lo : base + CH], in0=banks[idx][:, 0:nw], scalar=1.0,
+                    in1=urows[t][:, uo : uo + nw], op0=ALU.mult, op1=ALU.mult,
+                    accum_out=accds[t][:, NC + c : NC + c + 1],
+                )
+                if idx == 0:
+                    small_a(t - 1)
+                if idx == 1:
+                    small_b(t - 1)
+                if idx + 3 < len(units):
+                    banks.append(fill_tv(t, units[idx + 3]))
+            if len(units) == 1:
+                small_b(t - 1)
+
+        def stage_w(t):
+            if not live(t):
+                return
+            x0 = CEN - P * (t % NT)
+            wl = []
+            for c in range(NC):
+                w = work.tile([P, CH], F32, tag="w", bufs=8)
+                nc.gpsimd.tensor_tensor(out=w[:], in0=kch[t][c], in1=tab[:, x0 + CH * c : x0 + CH * (c + 1)], op=ALU.mult)
+                wl.append(w)
+            wch[t] = wl
+            pbs[t] = []
+
+        def stage_p(t, c):
+            if not live(t):
+                return
+            b, i = divmod(t, NT)
+            pb = psp.tile([P, CH], F32, tag="p")
+            nc.tensor.matmul_mx(
+                out=pb[:],
+                lhsT=gc[b][:, P * i : P * (i + 1)].bitcast(E5X4), lhsT_scale=gs[b][:, P * i : P * (i + 1)],
+                rhs=lc[b][:, CH * c : CH * (c + 1)].bitcast(E4X4), rhs_scale=ls[b][:, CH * c : CH * (c + 1)],
+                start=True, stop=True,
+            )
+            pbs[t].append(pb)
+
+        def one_x(t, c):
+            nc.vector.scalar_tensor_tensor(
+                out=junk[:], in0=pbs[t][c][:], scalar=1.0, in1=kch[t][c], op0=ALU.mult, op1=ALU.mult,
+                accum_out=accds[t][:, c : c + 1],
+            )
+
+        def x_phase(t):
+            if not live(t):
+                return
+            i = t % NT
+            c0, m = divmod(i, 4)
+            na = c0 + (1 if m > 0 else 0)
+            if c0 == NC - 1:
+                sd = accds[t][:, 2 * NC - 1 : 2 * NC]
+            else:
+                sdt = small.tile([P, 1], F32, tag="sdt")
+                nc.vector.tensor_reduce(out=sdt[:], in_=accds[t][:, NC + c0 : 2 * NC], axis=AX.X, op=ALU.add)
+                sd = sdt[:, 0:1]
+            if na > 1:
+                sast = small.tile([P, 1], F32, tag="sas")
+                nc.vector.tensor_reduce(out=sast[:], in_=accas[t][:, 0:na], axis=AX.X, op=ALU.add)
+            one_x(t, 0)
+            tot = small.tile([P, 1], F32, tag="tot")
+            if na == 0:
+                nc.vector.tensor_scalar(out=tot[:], in0=sd, scalar1=1e-8, scalar2=None, op0=ALU.add)
+            else:
+                sas = sast[:, 0:1] if na > 1 else accas[t][:, 0:1]
+                nc.vector.tensor_scalar(out=tot[:], in0=sd, scalar1=sas, scalar2=1e-8, op0=ALU.add, op1=ALU.add)
+            one_x(t, 1)
+            sig = small.tile([P, 1], F32, tag="sig")
+            nc.vector.reciprocal(out=sig[:], in_=tot[:])
+            sigs[t] = sig
+            one_x(t, 2)
+            nc.vector.tensor_scalar(out=ws[:, t : t + 1], in0=sig[:], scalar1=-0.5, scalar2=None, op0=ALU.mult)
+            one_x(t, 3)
+
+        def stage_h(t, c):
+            h = work.tile([P, CH], F32, tag="h", bufs=3)
+            nc.vector.scalar_tensor_tensor(
+                out=h[:], in0=pbs[t][c][:], scalar=negcs[t][:, 0:1], in1=wch[t][c][:], op0=ALU.add, op1=ALU.mult,
+                accum_out=rpart[:, NC * t + c : NC * t + c + 1],
+            )
+            return h
+
+        def stage_mv(t, c, h):
+            for q in range(4):
+                col = NT * t + 4 * c + q
+                nc.tensor.matmul(
+                    out=cacc[:, col : col + 1], lhsT=h[:, P * q : P * (q + 1)], rhs=ws[:, t : t + 1], start=True, stop=True
+                )
+
+        for n in range(3):
+            g_load(n)
+        stage_u(0)
+        stage_u(1)
+        for n in range(HEAD):
+            g_tr(n, True)
+            g_load(n + 3)
+            if n > 0:
+                g_q(n - 1)
+        g_q(HEAD - 1)
+        pool_ud(0)
+        prefetch(0)
+        for s in range(-1, STEPS):
+            k_phase(s + 1)
+            pool_ud(s + 2)
+            stage_w(s + 1)
+            n = HEAD + s
+            if s >= 0 and n <= len(groups):
+                if n > HEAD:
+                    g_q(n - 1)
+                if n < len(groups):
+                    g_tr(n, False)
+                    g_load(n + 3)
+            for c in range(NC):
+                if s >= 0:
+                    h = stage_h(s, c)
+                stage_p(s + 1, c)
+                if s >= 0:
+                    stage_mv(s, c, h)
+            x_phase(s + 1)
+            prefetch(s + 2)
+            stage_u(s + 3)
+
+        rs = const.tile([P, STEPS], F32)
+        nc.vector.tensor_reduce(out=rs[:], in_=rpart[:].rearrange("p (t c) -> p t c", c=NC), axis=AX.X, op=ALU.add)
+        cs = const.tile([P, STEPS], F32)
+        nc.vector.tensor_reduce(
+            out=cs[:].rearrange("p (b j) -> p b j", b=B), in_=cacc[:].rearrange("p (b i j) -> p b j i", b=B, i=NT),
+            axis=AX.X, op=ALU.add,
+        )
+        fin = const.tile([P, P], F32)
+        nc.vector.memset(fin[:], 0.0)
+        nc.vector.tensor_tensor(out=rs[:], in0=rs[:], in1=ws[:], op=ALU.mult)
+        nc.vector.tensor_tensor(out=fin[:, 0:STEPS], in0=rs[:], in1=cs[:], op=ALU.add)
+        fps = pst.tile([P, CH], F32, tag="tp")
+        nc.tensor.transpose(fps[:, 0:P], fin[:], ident[:])
+        osb = const.tile([P, P], F32)
+        nc.vector.tensor_copy(out=osb[:], in_=fps[:, 0:P])
+        nc.sync.dma_start(out=out.rearrange("b (t p) -> (b t) p", p=P), in_=osb[0:STEPS, :])

@@ -40,8 +40,7 @@ def tile_csocrgattention_kernel(tc, latent, alpha, grad_out, out):
         upool = ctx.enter_context(tc.tile_pool(name="upool", bufs=2))
         work = ctx.enter_context(tc.tile_pool(name="work", bufs=3))
         small = ctx.enter_context(tc.tile_pool(name="small", bufs=3))
-        psp = ctx.enter_context(tc.psum_pool(name="psp", bufs=4))
-        pst = ctx.enter_context(tc.psum_pool(name="pst", bufs=3))
+        pst = ctx.enter_context(tc.psum_pool(name="pst", bufs=4))
         psc = ctx.enter_context(tc.psum_pool(name="psc", bufs=1))
         ctx.enter_context(tc.manual_schedule())
 
@@ -104,7 +103,8 @@ def tile_csocrgattention_kernel(tc, latent, alpha, grad_out, out):
 
         ws = const.tile([P, STEPS], F32)
         rpart = const.tile([P, STEPS * NC], F32)
-        cacc = psc.tile([P, CH], F32)
+        cs = const.tile([P, STEPS], F32)
+        caccs = {}
         junk = const.tile([P, CH], F32)
 
         gc = [codes.tile([P, N], U32, name="gc%d" % b, align_bytes=64) for b in range(B)]
@@ -121,7 +121,7 @@ def tile_csocrgattention_kernel(tc, latent, alpha, grad_out, out):
         def g_load(n):
             if n < len(groups):
                 src, b, g = groups[n][0:3]
-                xsb = stage.tile([P, 4, D], BF16, tag="xsb", bufs=3)
+                xsb = stage.tile([P, 4, D], BF16, tag="xsb", bufs=2)
                 nc.sync.dma_start(out=xsb[:], in_=src[b, CH * g : CH * (g + 1), :].rearrange("(a p) d -> p a d", p=P))
                 xsbs[n] = xsb
 
@@ -154,7 +154,6 @@ def tile_csocrgattention_kernel(tc, latent, alpha, grad_out, out):
         ulcs = {}
         kch = {}
         wch = {}
-        pbs = {}
         accds = {}
         accas = {}
         sigs = {}
@@ -175,6 +174,13 @@ def tile_csocrgattention_kernel(tc, latent, alpha, grad_out, out):
             nc.scalar.activation(out=ud0[:], in_=tab[:, CEN:R0], func=ACT.Exp, scale=sc)
             urows[t] = urow
             ud0s[t] = ud0
+
+        def stage_u_rest(t):
+            if not live(t):
+                return
+            b, i = divmod(t, NT)
+            urow = urows[t]
+            sc = nega[:, t : t + 1]
             if i < NT - 1:
                 ulc = upool.tile([P, N - P], F32, tag="ulc")
                 for j in range(i + 1, NT):
@@ -238,8 +244,7 @@ def tile_csocrgattention_kernel(tc, latent, alpha, grad_out, out):
             for c in range(c0, NC):
                 chunks.append(kpi[:, CH * (c - c0) : CH * (c - c0 + 1)])
             kch[t] = chunks
-            units = [(c, m if c == c0 else 0) for c in range(c0, NC)]
-            tvs[t] = [units, [fill_tv(t, un) for un in units[0:3]]]
+            tvs[t] = [(c, m if c == c0 else 0) for c in range(c0, NC)]
 
         def small_a(t):
             if live(t):
@@ -262,14 +267,15 @@ def tile_csocrgattention_kernel(tc, latent, alpha, grad_out, out):
                 return
             i = t % NT
             c0 = i // 4
-            units, banks = tvs[t]
+            units = tvs[t]
             for idx in range(len(units)):
                 c, lo = units[idx]
+                bank = fill_tv(t, units[idx])
                 nw = P * (4 - lo)
                 uo = P * (4 * c + lo - i)
                 base = CH * (c - c0)
                 nc.vector.scalar_tensor_tensor(
-                    out=kp[i][:, base + P * lo : base + CH], in0=banks[idx][:, 0:nw], scalar=1.0,
+                    out=kp[i][:, base + P * lo : base + CH], in0=bank[:, 0:nw], scalar=1.0,
                     in1=urows[t][:, uo : uo + nw], op0=ALU.mult, op1=ALU.mult,
                     accum_out=accds[t][:, NC + c : NC + c + 1],
                 )
@@ -277,8 +283,6 @@ def tile_csocrgattention_kernel(tc, latent, alpha, grad_out, out):
                     small_a(t - 1)
                 if idx == 1:
                     small_b(t - 1)
-                if idx + 3 < len(units):
-                    banks.append(fill_tv(t, units[idx + 3]))
             if len(units) == 1:
                 small_b(t - 1)
 
@@ -292,24 +296,40 @@ def tile_csocrgattention_kernel(tc, latent, alpha, grad_out, out):
                 nc.gpsimd.tensor_tensor(out=w[:], in0=kch[t][c], in1=tab[:, x0 + CH * c : x0 + CH * (c + 1)], op=ALU.mult)
                 wl.append(w)
             wch[t] = wl
-            pbs[t] = []
 
         def stage_p(t, c):
-            if not live(t):
-                return
             b, i = divmod(t, NT)
-            pb = psp.tile([P, CH], F32, tag="p")
+            pb = pst.tile([P, CH], F32, tag="tp")
             nc.tensor.matmul_mx(
                 out=pb[:],
                 lhsT=gc[b][:, P * i : P * (i + 1)].bitcast(E5X4), lhsT_scale=gs[b][:, P * i : P * (i + 1)],
                 rhs=lc[b][:, CH * c : CH * (c + 1)].bitcast(E4X4), rhs_scale=ls[b][:, CH * c : CH * (c + 1)],
                 start=True, stop=True,
             )
-            pbs[t].append(pb)
+            return pb
+
+        pending = {}
+
+        def flush_ht(c):
+            if pending.get(c) is None:
+                return
+            t, h = pending[c]
+            pending[c] = None
+            i = t % NT
+            if i == 0:
+                cacc = psc.tile([P, CH], F32, tag="ca%d" % c, name="ca%d_%d" % (c, t))
+                caccs[c] = cacc
+            for q in range(4):
+                nc.tensor.matmul(
+                    out=caccs[c][:, P * q : P * (q + 1)], lhsT=h[:, P * q : P * (q + 1)], rhs=ident[:], is_transpose=True,
+                    start=(i == 0 and q == 0), stop=(i == NT - 1 and q == 3),
+                )
 
         def one_x(t, c):
+            pb = stage_p(t, c)
+            flush_ht(c)
             nc.vector.scalar_tensor_tensor(
-                out=junk[:], in0=pbs[t][c][:], scalar=1.0, in1=kch[t][c], op0=ALU.mult, op1=ALU.mult,
+                out=junk[:], in0=pb[:], scalar=1.0, in1=kch[t][c], op0=ALU.mult, op1=ALU.mult,
                 accum_out=accds[t][:, c : c + 1],
             )
 
@@ -344,60 +364,59 @@ def tile_csocrgattention_kernel(tc, latent, alpha, grad_out, out):
             one_x(t, 3)
 
         def stage_h(t, c):
-            h = work.tile([P, CH], F32, tag="h", bufs=3)
+            pb = stage_p(t, c)
+            h = work.tile([P, CH], F32, tag="h", bufs=6)
             nc.vector.scalar_tensor_tensor(
-                out=h[:], in0=pbs[t][c][:], scalar=negcs[t][:, 0:1], in1=wch[t][c][:], op0=ALU.add, op1=ALU.mult,
+                out=h[:], in0=pb[:], scalar=negcs[t][:, 0:1], in1=wch[t][c][:], op0=ALU.add, op1=ALU.mult,
                 accum_out=rpart[:, NC * t + c : NC * t + c + 1],
             )
-            return h
+            nc.scalar.activation(out=h[:], in_=h[:], func=ACT.Copy, scale=ws[:, t : t + 1])
+            pending[c] = (t, h)
 
-        def stage_mv(t, c, h):
-            for q in range(4):
-                col = NT * t + 4 * c + q
-                nc.tensor.matmul(
-                    out=cacc[:, col : col + 1], lhsT=h[:, P * q : P * (q + 1)], rhs=ws[:, t : t + 1], start=True, stop=True
+        def read_c(b):
+            for c in range(NC):
+                nc.vector.tensor_reduce(
+                    out=cs[:, NT * b + 4 * c : NT * b + 4 * (c + 1)],
+                    in_=caccs[c][:].rearrange("p (q r) -> p q r", q=4), axis=AX.X, op=ALU.add,
                 )
 
-        for n in range(3):
+        for n in range(2):
             g_load(n)
         stage_u(0)
-        stage_u(1)
+        stage_u_rest(0)
         for n in range(HEAD):
             g_tr(n, True)
-            g_load(n + 3)
+            g_load(n + 2)
             if n > 0:
                 g_q(n - 1)
         g_q(HEAD - 1)
         pool_ud(0)
-        prefetch(0)
-        for s in range(-1, STEPS):
-            k_phase(s + 1)
-            pool_ud(s + 2)
-            stage_w(s + 1)
-            n = HEAD + s
-            if s >= 0 and n <= len(groups):
+        for s in range(-2, STEPS - 1):
+            if s == NT:
+                read_c(0)
+            stage_u(s + 3)
+            x_phase(s + 1)
+            prefetch(s + 2)
+            pool_ud(s + 3)
+            k_phase(s + 2)
+            stage_w(s + 2)
+            n = HEAD + s + 2
+            if n <= len(groups):
                 if n > HEAD:
                     g_q(n - 1)
                 if n < len(groups):
                     g_tr(n, False)
-                    g_load(n + 3)
-            for c in range(NC):
-                if s >= 0:
-                    h = stage_h(s, c)
-                stage_p(s + 1, c)
-                if s >= 0:
-                    stage_mv(s, c, h)
-            x_phase(s + 1)
-            prefetch(s + 2)
-            stage_u(s + 3)
+                    g_load(n + 2)
+            stage_u_rest(s + 3)
+            if live(s + 1):
+                for c in range(NC):
+                    stage_h(s + 1, c)
+        for c in range(NC):
+            flush_ht(c)
+        read_c(1)
 
         rs = const.tile([P, STEPS], F32)
         nc.vector.tensor_reduce(out=rs[:], in_=rpart[:].rearrange("p (t c) -> p t c", c=NC), axis=AX.X, op=ALU.add)
-        cs = const.tile([P, STEPS], F32)
-        nc.vector.tensor_reduce(
-            out=cs[:].rearrange("p (b j) -> p b j", b=B), in_=cacc[:].rearrange("p (b i j) -> p b j i", b=B, i=NT),
-            axis=AX.X, op=ALU.add,
-        )
         fin = const.tile([P, P], F32)
         nc.vector.memset(fin[:], 0.0)
         nc.vector.tensor_tensor(out=rs[:], in0=rs[:], in1=ws[:], op=ALU.mult)

@@ -212,7 +212,7 @@ def tile_csocrgattention_kernel(tc, latent, alpha, grad_out, out):
                 nc.tensor.transpose(vt[:, P * (q - lo) : P * (q - lo + 1)], srcb, ident[:])
             return vt
 
-        def prefetch(t):
+        def alloc_step(t):
             if not live(t):
                 return
             b, i = divmod(t, NT)
@@ -224,33 +224,46 @@ def tile_csocrgattention_kernel(tc, latent, alpha, grad_out, out):
             if i > 0:
                 acca = small.tile([P, NC], F32, tag="acca")
                 accas[t] = acca
-            chunks = []
-            for c in range(c0):
-                kt = pst.tile([P, CH], F32, tag="tp")
-                for q in range(4):
-                    j = 4 * c + q
-                    off = P * i - CH * (j // 4)
-                    nc.tensor.transpose(kt[:, P * q : P * (q + 1)], kp[j][:, off : off + P], ident[:])
-                klo = work.tile([P, CH], F32, tag="klo", bufs=6)
-                nc.scalar.activation(out=klo[:], in_=kt[:], func=ACT.Copy, accum_out=acca[:, c : c + 1])
-                chunks.append(klo[:])
-            if m > 0:
-                kt = pst.tile([P, CH], F32, tag="tp")
-                for q in range(m):
-                    nc.tensor.transpose(kt[:, P * q : P * (q + 1)], kp[4 * c0 + q][:, P * m : P * (m + 1)], ident[:])
-                nc.scalar.activation(
-                    out=kpi[:, 0 : P * m], in_=kt[:, 0 : P * m], func=ACT.Copy, accum_out=acca[:, c0 : c0 + 1]
-                )
-            for c in range(c0, NC):
-                chunks.append(kpi[:, CH * (c - c0) : CH * (c - c0 + 1)])
-            kch[t] = chunks
+            kch[t] = [None] * c0 + [kpi[:, CH * (c - c0) : CH * (c - c0 + 1)] for c in range(c0, NC)]
+            wch[t] = [None] * NC
             tvs[t] = [(c, m if c == c0 else 0) for c in range(c0, NC)]
+
+        def n_tk(t):
+            if not live(t):
+                return 0
+            c0, m = divmod(t % NT, 4)
+            return c0 + (1 if m > 0 else 0)
+
+        def tk_unit(t, c):
+            i = t % NT
+            c0, m = divmod(i, 4)
+            nb = 4 if c < c0 else m
+            kt = pst.tile([P, CH], F32, tag="tp")
+            for q in range(nb):
+                j = 4 * c + q
+                off = P * i - CH * c
+                nc.tensor.transpose(kt[:, P * q : P * (q + 1)], kp[j][:, off : off + P], ident[:])
+            if c < c0:
+                klo = work.tile([P, CH], F32, tag="klo", bufs=6)
+                dst = klo[:]
+                kch[t][c] = dst
+            else:
+                dst = kp[i][:, 0 : P * m]
+            nc.scalar.activation(out=dst, in_=kt[:, 0 : P * nb], func=ACT.Copy, accum_out=accas[t][:, c : c + 1])
+            one_w(t, c)
+
+        def one_w(t, c):
+            x0 = CEN - P * (t % NT)
+            w = work.tile([P, CH], F32, tag="w", bufs=8)
+            nc.gpsimd.tensor_tensor(out=w[:], in0=kch[t][c], in1=tab[:, x0 + CH * c : x0 + CH * (c + 1)], op=ALU.mult)
+            wch[t][c] = w
 
         def small_a(t):
             if live(t):
                 ared = small.tile([P, 1], F32, tag="ared")
                 nc.vector.tensor_reduce(out=ared[:], in_=accds[t][:, 0:NC], axis=AX.X, op=ALU.add)
                 areds[t] = ared
+                nc.vector.tensor_scalar(out=ws[:, t : t + 1], in0=sigs[t][:], scalar1=-0.5, scalar2=None, op0=ALU.mult)
 
         def small_b(t):
             if live(t):
@@ -259,54 +272,6 @@ def tile_csocrgattention_kernel(tc, latent, alpha, grad_out, out):
                     out=negc[:], in0=areds[t][:], scalar1=sigs[t][:, 0:1], scalar2=-1.0, op0=ALU.mult, op1=ALU.mult
                 )
                 negcs[t] = negc
-
-        def k_phase(t):
-            if not live(t):
-                small_a(t - 1)
-                small_b(t - 1)
-                return
-            i = t % NT
-            c0 = i // 4
-            units = tvs[t]
-            for idx in range(len(units)):
-                c, lo = units[idx]
-                bank = fill_tv(t, units[idx])
-                nw = P * (4 - lo)
-                uo = P * (4 * c + lo - i)
-                base = CH * (c - c0)
-                nc.vector.scalar_tensor_tensor(
-                    out=kp[i][:, base + P * lo : base + CH], in0=bank[:, 0:nw], scalar=1.0,
-                    in1=urows[t][:, uo : uo + nw], op0=ALU.mult, op1=ALU.mult,
-                    accum_out=accds[t][:, NC + c : NC + c + 1],
-                )
-                if idx == 0:
-                    small_a(t - 1)
-                if idx == 1:
-                    small_b(t - 1)
-            if len(units) == 1:
-                small_b(t - 1)
-
-        def stage_w(t):
-            if not live(t):
-                return
-            x0 = CEN - P * (t % NT)
-            wl = []
-            for c in range(NC):
-                w = work.tile([P, CH], F32, tag="w", bufs=8)
-                nc.gpsimd.tensor_tensor(out=w[:], in0=kch[t][c], in1=tab[:, x0 + CH * c : x0 + CH * (c + 1)], op=ALU.mult)
-                wl.append(w)
-            wch[t] = wl
-
-        def stage_p(t, c):
-            b, i = divmod(t, NT)
-            pb = pst.tile([P, CH], F32, tag="tp")
-            nc.tensor.matmul_mx(
-                out=pb[:],
-                lhsT=gc[b][:, P * i : P * (i + 1)].bitcast(E5X4), lhsT_scale=gs[b][:, P * i : P * (i + 1)],
-                rhs=lc[b][:, CH * c : CH * (c + 1)].bitcast(E4X4), rhs_scale=ls[b][:, CH * c : CH * (c + 1)],
-                start=True, stop=True,
-            )
-            return pb
 
         pending = {}
 
@@ -325,9 +290,51 @@ def tile_csocrgattention_kernel(tc, latent, alpha, grad_out, out):
                     start=(i == 0 and q == 0), stop=(i == NT - 1 and q == 3),
                 )
 
-        def one_x(t, c):
-            pb = stage_p(t, c)
-            flush_ht(c)
+        def k_phase(t):
+            if not live(t):
+                flush_ht(2)
+                flush_ht(3)
+                small_a(t - 1)
+                small_b(t - 1)
+                return
+            i = t % NT
+            c0, m = divmod(i, 4)
+            units = tvs[t]
+            for idx in range(len(units)):
+                c, lo = units[idx]
+                bank = fill_tv(t, units[idx])
+                if idx < 2:
+                    flush_ht(2 + idx)
+                nw = P * (4 - lo)
+                uo = P * (4 * c + lo - i)
+                base = CH * (c - c0)
+                nc.vector.scalar_tensor_tensor(
+                    out=kp[i][:, base + P * lo : base + CH], in0=bank[:, 0:nw], scalar=1.0,
+                    in1=urows[t][:, uo : uo + nw], op0=ALU.mult, op1=ALU.mult,
+                    accum_out=accds[t][:, NC + c : NC + c + 1],
+                )
+                if idx == 0:
+                    small_a(t - 1)
+                if idx == 1:
+                    small_b(t - 1)
+                if lo == 0:
+                    one_w(t, c)
+            flush_ht(3)
+            if len(units) == 1:
+                small_b(t - 1)
+
+        def stage_p(t, c):
+            b, i = divmod(t, NT)
+            pb = pst.tile([P, CH], F32, tag="tp")
+            nc.tensor.matmul_mx(
+                out=pb[:],
+                lhsT=gc[b][:, P * i : P * (i + 1)].bitcast(E5X4), lhsT_scale=gs[b][:, P * i : P * (i + 1)],
+                rhs=lc[b][:, CH * c : CH * (c + 1)].bitcast(E4X4), rhs_scale=ls[b][:, CH * c : CH * (c + 1)],
+                start=True, stop=True,
+            )
+            return pb
+
+        def one_x(t, c, pb):
             nc.vector.scalar_tensor_tensor(
                 out=junk[:], in0=pb[:], scalar=1.0, in1=kch[t][c], op0=ALU.mult, op1=ALU.mult,
                 accum_out=accds[t][:, c : c + 1],
@@ -335,10 +342,17 @@ def tile_csocrgattention_kernel(tc, latent, alpha, grad_out, out):
 
         def x_phase(t):
             if not live(t):
+                flush_ht(0)
+                flush_ht(1)
                 return
             i = t % NT
             c0, m = divmod(i, 4)
             na = c0 + (1 if m > 0 else 0)
+            pbl = [stage_p(t, c) for c in range(NC)]
+            flush_ht(0)
+            flush_ht(1)
+            one_x(t, 0, pbl[0])
+            one_x(t, 1, pbl[1])
             if c0 == NC - 1:
                 sd = accds[t][:, 2 * NC - 1 : 2 * NC]
             else:
@@ -348,30 +362,32 @@ def tile_csocrgattention_kernel(tc, latent, alpha, grad_out, out):
             if na > 1:
                 sast = small.tile([P, 1], F32, tag="sas")
                 nc.vector.tensor_reduce(out=sast[:], in_=accas[t][:, 0:na], axis=AX.X, op=ALU.add)
-            one_x(t, 0)
+            one_x(t, 2, pbl[2])
             tot = small.tile([P, 1], F32, tag="tot")
             if na == 0:
                 nc.vector.tensor_scalar(out=tot[:], in0=sd, scalar1=1e-8, scalar2=None, op0=ALU.add)
             else:
                 sas = sast[:, 0:1] if na > 1 else accas[t][:, 0:1]
                 nc.vector.tensor_scalar(out=tot[:], in0=sd, scalar1=sas, scalar2=1e-8, op0=ALU.add, op1=ALU.add)
-            one_x(t, 1)
+            one_x(t, 3, pbl[3])
             sig = small.tile([P, 1], F32, tag="sig")
             nc.vector.reciprocal(out=sig[:], in_=tot[:])
             sigs[t] = sig
-            one_x(t, 2)
-            nc.vector.tensor_scalar(out=ws[:, t : t + 1], in0=sig[:], scalar1=-0.5, scalar2=None, op0=ALU.mult)
-            one_x(t, 3)
 
-        def stage_h(t, c):
-            pb = stage_p(t, c)
-            h = work.tile([P, CH], F32, tag="h", bufs=6)
-            nc.vector.scalar_tensor_tensor(
-                out=h[:], in0=pb[:], scalar=negcs[t][:, 0:1], in1=wch[t][c][:], op0=ALU.add, op1=ALU.mult,
-                accum_out=rpart[:, NC * t + c : NC * t + c + 1],
-            )
-            nc.scalar.activation(out=h[:], in_=h[:], func=ACT.Copy, scale=ws[:, t : t + 1])
-            pending[c] = (t, h)
+        def h_phase(t, t2):
+            if live(t):
+                pbl = [stage_p(t, c) for c in range(NC)]
+            for c in range(NC):
+                if live(t):
+                    h = work.tile([P, CH], F32, tag="h", bufs=6)
+                    nc.vector.scalar_tensor_tensor(
+                        out=h[:], in0=pbl[c][:], scalar=negcs[t][:, 0:1], in1=wch[t][c][:], op0=ALU.add, op1=ALU.mult,
+                        accum_out=rpart[:, NC * t + c : NC * t + c + 1],
+                    )
+                    nc.scalar.activation(out=h[:], in_=h[:], func=ACT.Copy, scale=ws[:, t : t + 1])
+                    pending[c] = (t, h)
+                if c < n_tk(t2):
+                    tk_unit(t2, c)
 
         def read_c(b):
             for c in range(NC):
@@ -395,22 +411,18 @@ def tile_csocrgattention_kernel(tc, latent, alpha, grad_out, out):
             if s == NT:
                 read_c(0)
             stage_u(s + 3)
+            stage_u_rest(s + 3)
             x_phase(s + 1)
-            prefetch(s + 2)
+            alloc_step(s + 2)
             pool_ud(s + 3)
             k_phase(s + 2)
-            stage_w(s + 2)
             n = HEAD + s + 2
-            if n <= len(groups):
-                if n > HEAD:
-                    g_q(n - 1)
-                if n < len(groups):
-                    g_tr(n, False)
-                    g_load(n + 2)
-            stage_u_rest(s + 3)
-            if live(s + 1):
-                for c in range(NC):
-                    stage_h(s + 1, c)
+            if HEAD < n <= len(groups):
+                g_q(n - 1)
+            h_phase(s + 1, s + 2)
+            if n < len(groups):
+                g_tr(n, False)
+                g_load(n + 2)
         for c in range(NC):
             flush_ht(c)
         read_c(1)

@@ -155,8 +155,6 @@ def tile_csocrgattention_kernel(tc, latent, alpha, grad_out, out):
         kch = {}
         wch = {}
         accds = {}
-        accas = {}
-        sigs = {}
         negcs = {}
         areds = {}
         tvs = {}
@@ -219,11 +217,8 @@ def tile_csocrgattention_kernel(tc, latent, alpha, grad_out, out):
             c0, m = divmod(i, 4)
             kpi = kpool.tile([P, N - CH * c0], F32, tag="kp%d" % i, name="kp%d_%d" % (i, b))
             kp[i] = kpi
-            accd = small.tile([P, 2 * NC], F32, tag="accd")
+            accd = small.tile([P, 24], F32, tag="accd")
             accds[t] = accd
-            if i > 0:
-                acca = small.tile([P, NC], F32, tag="acca")
-                accas[t] = acca
             kch[t] = [None] * c0 + [kpi[:, CH * (c - c0) : CH * (c - c0 + 1)] for c in range(c0, NC)]
             wch[t] = [None] * NC
             tvs[t] = [(c, m if c == c0 else 0) for c in range(c0, NC)]
@@ -249,7 +244,7 @@ def tile_csocrgattention_kernel(tc, latent, alpha, grad_out, out):
                 kch[t][c] = dst
             else:
                 dst = kp[i][:, 0 : P * m]
-            nc.scalar.activation(out=dst, in_=kt[:, 0 : P * nb], func=ACT.Copy, accum_out=accas[t][:, c : c + 1])
+            nc.scalar.activation(out=dst, in_=kt[:, 0 : P * nb], func=ACT.Copy, accum_out=accds[t][:, 16 + c : 17 + c])
             one_w(t, c)
 
         def one_w(t, c):
@@ -263,13 +258,12 @@ def tile_csocrgattention_kernel(tc, latent, alpha, grad_out, out):
                 ared = small.tile([P, 1], F32, tag="ared")
                 nc.vector.tensor_reduce(out=ared[:], in_=accds[t][:, 0:NC], axis=AX.X, op=ALU.add)
                 areds[t] = ared
-                nc.vector.tensor_scalar(out=ws[:, t : t + 1], in0=sigs[t][:], scalar1=-0.5, scalar2=None, op0=ALU.mult)
 
         def small_b(t):
             if live(t):
                 negc = small.tile([P, 1], F32, tag="negc")
                 nc.vector.tensor_scalar(
-                    out=negc[:], in0=areds[t][:], scalar1=sigs[t][:, 0:1], scalar2=-1.0, op0=ALU.mult, op1=ALU.mult
+                    out=negc[:], in0=areds[t][:], scalar1=ws[:, t : t + 1], scalar2=2.0, op0=ALU.mult, op1=ALU.mult
                 )
                 negcs[t] = negc
 
@@ -311,7 +305,7 @@ def tile_csocrgattention_kernel(tc, latent, alpha, grad_out, out):
                 nc.vector.scalar_tensor_tensor(
                     out=kp[i][:, base + P * lo : base + CH], in0=bank[:, 0:nw], scalar=1.0,
                     in1=urows[t][:, uo : uo + nw], op0=ALU.mult, op1=ALU.mult,
-                    accum_out=accds[t][:, NC + c : NC + c + 1],
+                    accum_out=accds[t][:, 12 + c : 13 + c],
                 )
                 if idx == 0:
                     small_a(t - 1)
@@ -353,26 +347,13 @@ def tile_csocrgattention_kernel(tc, latent, alpha, grad_out, out):
             flush_ht(1)
             one_x(t, 0, pbl[0])
             one_x(t, 1, pbl[1])
-            if c0 == NC - 1:
-                sd = accds[t][:, 2 * NC - 1 : 2 * NC]
-            else:
-                sdt = small.tile([P, 1], F32, tag="sdt")
-                nc.vector.tensor_reduce(out=sdt[:], in_=accds[t][:, NC + c0 : 2 * NC], axis=AX.X, op=ALU.add)
-                sd = sdt[:, 0:1]
-            if na > 1:
-                sast = small.tile([P, 1], F32, tag="sas")
-                nc.vector.tensor_reduce(out=sast[:], in_=accas[t][:, 0:na], axis=AX.X, op=ALU.add)
+            sred = small.tile([P, 1], F32, tag="sred")
+            nc.vector.tensor_reduce(out=sred[:], in_=accds[t][:, 12 + c0 : 16 + na], axis=AX.X, op=ALU.add)
             one_x(t, 2, pbl[2])
             tot = small.tile([P, 1], F32, tag="tot")
-            if na == 0:
-                nc.vector.tensor_scalar(out=tot[:], in0=sd, scalar1=1e-8, scalar2=None, op0=ALU.add)
-            else:
-                sas = sast[:, 0:1] if na > 1 else accas[t][:, 0:1]
-                nc.vector.tensor_scalar(out=tot[:], in0=sd, scalar1=sas, scalar2=1e-8, op0=ALU.add, op1=ALU.add)
+            nc.vector.tensor_scalar(out=tot[:], in0=sred[:], scalar1=-2.0, scalar2=-2e-8, op0=ALU.mult, op1=ALU.add)
             one_x(t, 3, pbl[3])
-            sig = small.tile([P, 1], F32, tag="sig")
-            nc.vector.reciprocal(out=sig[:], in_=tot[:])
-            sigs[t] = sig
+            nc.vector.reciprocal(out=ws[:, t : t + 1], in_=tot[:])
 
         def h_phase(t, t2):
             if live(t):
@@ -382,12 +363,12 @@ def tile_csocrgattention_kernel(tc, latent, alpha, grad_out, out):
                     h = work.tile([P, CH], F32, tag="h", bufs=6)
                     nc.vector.scalar_tensor_tensor(
                         out=h[:], in0=pbl[c][:], scalar=negcs[t][:, 0:1], in1=wch[t][c][:], op0=ALU.add, op1=ALU.mult,
+                    )
+                    nc.scalar.activation(
+                        out=h[:], in_=h[:], func=ACT.Copy, scale=ws[:, t : t + 1],
                         accum_out=rpart[:, NC * t + c : NC * t + c + 1],
                     )
-                    nc.scalar.activation(out=h[:], in_=h[:], func=ACT.Copy, scale=ws[:, t : t + 1])
                     pending[c] = (t, h)
-                if c < n_tk(t2):
-                    tk_unit(t2, c)
 
         def read_c(b):
             for c in range(NC):
@@ -416,6 +397,8 @@ def tile_csocrgattention_kernel(tc, latent, alpha, grad_out, out):
             alloc_step(s + 2)
             pool_ud(s + 3)
             k_phase(s + 2)
+            for c in range(n_tk(s + 2)):
+                tk_unit(s + 2, c)
             n = HEAD + s + 2
             if HEAD < n <= len(groups):
                 g_q(n - 1)
@@ -431,7 +414,6 @@ def tile_csocrgattention_kernel(tc, latent, alpha, grad_out, out):
         nc.vector.tensor_reduce(out=rs[:], in_=rpart[:].rearrange("p (t c) -> p t c", c=NC), axis=AX.X, op=ALU.add)
         fin = const.tile([P, P], F32)
         nc.vector.memset(fin[:], 0.0)
-        nc.vector.tensor_tensor(out=rs[:], in0=rs[:], in1=ws[:], op=ALU.mult)
         nc.vector.tensor_tensor(out=fin[:, 0:STEPS], in0=rs[:], in1=cs[:], op=ALU.add)
         fps = pst.tile([P, CH], F32, tag="tp")
         nc.tensor.transpose(fps[:, 0:P], fin[:], ident[:])

@@ -106,6 +106,7 @@ def tile_csocrgattention_kernel(tc, latent, alpha, grad_out, out):
         cs = const.tile([P, STEPS], F32)
         caccs = {}
         junk = const.tile([P, CH], F32)
+        sjunk = const.tile([P, 8], F32)
 
         gc = [codes.tile([P, N], U32, name="gc%d" % b, align_bytes=64) for b in range(B)]
         gs = [codes.tile([P, N], U8, name="gs%d" % b, align_bytes=64) for b in range(B)]
@@ -156,7 +157,7 @@ def tile_csocrgattention_kernel(tc, latent, alpha, grad_out, out):
         wch = {}
         accds = {}
         negcs = {}
-        areds = {}
+        tots = {}
         tvs = {}
 
         def live(t):
@@ -253,17 +254,23 @@ def tile_csocrgattention_kernel(tc, latent, alpha, grad_out, out):
             nc.gpsimd.tensor_tensor(out=w[:], in0=kch[t][c], in1=tab[:, x0 + CH * c : x0 + CH * (c + 1)], op=ALU.mult)
             wch[t][c] = w
 
-        def small_a(t):
+        def small_s(t):
             if live(t):
-                ared = small.tile([P, 1], F32, tag="ared")
-                nc.vector.tensor_reduce(out=ared[:], in_=accds[t][:, 0:NC], axis=AX.X, op=ALU.add)
-                areds[t] = ared
+                c0, m = divmod(t % NT, 4)
+                na = c0 + (1 if m > 0 else 0)
+                n = NC - c0 + na
+                tot = small.tile([P, 1], F32, tag="tot")
+                nc.scalar.activation(
+                    out=sjunk[:, 0:n], in_=accds[t][:, 12 + c0 : 16 + na], func=ACT.Copy, scale=-1.0, bias=-1e-8 / n,
+                    accum_out=tot[:],
+                )
+                tots[t] = tot
 
-        def small_b(t):
+        def small_c(t):
             if live(t):
                 negc = small.tile([P, 1], F32, tag="negc")
-                nc.vector.tensor_scalar(
-                    out=negc[:], in0=areds[t][:], scalar1=ws[:, t : t + 1], scalar2=2.0, op0=ALU.mult, op1=ALU.mult
+                nc.scalar.activation(
+                    out=sjunk[:, 0:NC], in_=accds[t][:, 0:NC], func=ACT.Copy, scale=ws[:, t : t + 1], accum_out=negc[:],
                 )
                 negcs[t] = negc
 
@@ -288,8 +295,6 @@ def tile_csocrgattention_kernel(tc, latent, alpha, grad_out, out):
             if not live(t):
                 flush_ht(2)
                 flush_ht(3)
-                small_a(t - 1)
-                small_b(t - 1)
                 return
             i = t % NT
             c0, m = divmod(i, 4)
@@ -307,15 +312,9 @@ def tile_csocrgattention_kernel(tc, latent, alpha, grad_out, out):
                     in1=urows[t][:, uo : uo + nw], op0=ALU.mult, op1=ALU.mult,
                     accum_out=accds[t][:, 12 + c : 13 + c],
                 )
-                if idx == 0:
-                    small_a(t - 1)
-                if idx == 1:
-                    small_b(t - 1)
                 if lo == 0:
                     one_w(t, c)
             flush_ht(3)
-            if len(units) == 1:
-                small_b(t - 1)
 
         def stage_p(t, c):
             b, i = divmod(t, NT)
@@ -339,21 +338,14 @@ def tile_csocrgattention_kernel(tc, latent, alpha, grad_out, out):
                 flush_ht(0)
                 flush_ht(1)
                 return
-            i = t % NT
-            c0, m = divmod(i, 4)
-            na = c0 + (1 if m > 0 else 0)
             pbl = [stage_p(t, c) for c in range(NC)]
             flush_ht(0)
             flush_ht(1)
             one_x(t, 0, pbl[0])
+            nc.vector.reciprocal(out=ws[:, t : t + 1], in_=tots[t][:])
             one_x(t, 1, pbl[1])
-            sred = small.tile([P, 1], F32, tag="sred")
-            nc.vector.tensor_reduce(out=sred[:], in_=accds[t][:, 12 + c0 : 16 + na], axis=AX.X, op=ALU.add)
             one_x(t, 2, pbl[2])
-            tot = small.tile([P, 1], F32, tag="tot")
-            nc.vector.tensor_scalar(out=tot[:], in0=sred[:], scalar1=-2.0, scalar2=-2e-8, op0=ALU.mult, op1=ALU.add)
             one_x(t, 3, pbl[3])
-            nc.vector.reciprocal(out=ws[:, t : t + 1], in_=tot[:])
 
         def h_phase(t, t2):
             if live(t):
@@ -394,11 +386,13 @@ def tile_csocrgattention_kernel(tc, latent, alpha, grad_out, out):
             stage_u(s + 3)
             stage_u_rest(s + 3)
             x_phase(s + 1)
+            small_c(s + 1)
             alloc_step(s + 2)
             pool_ud(s + 3)
             k_phase(s + 2)
             for c in range(n_tk(s + 2)):
                 tk_unit(s + 2, c)
+            small_s(s + 2)
             n = HEAD + s + 2
             if HEAD < n <= len(groups):
                 g_q(n - 1)
@@ -418,5 +412,5 @@ def tile_csocrgattention_kernel(tc, latent, alpha, grad_out, out):
         fps = pst.tile([P, CH], F32, tag="tp")
         nc.tensor.transpose(fps[:, 0:P], fin[:], ident[:])
         osb = const.tile([P, P], F32)
-        nc.vector.tensor_copy(out=osb[:], in_=fps[:, 0:P])
+        nc.vector.tensor_scalar(out=osb[:], in0=fps[:, 0:P], scalar1=0.5, scalar2=None, op0=ALU.mult)
         nc.sync.dma_start(out=out.rearrange("b (t p) -> (b t) p", p=P), in_=osb[0:STEPS, :])

@@ -26,6 +26,7 @@ LAM = 64.0
 CEN = N - P
 TABW = 2 * N - P
 STEPS = B * NT
+GC = 0
 
 FLOPS = 2 * B * N * N * D
 
@@ -40,7 +41,7 @@ def tile_csocrgattention_kernel(tc, latent, alpha, grad_out, out):
         upool = ctx.enter_context(tc.tile_pool(name="upool", bufs=2))
         work = ctx.enter_context(tc.tile_pool(name="work", bufs=3))
         small = ctx.enter_context(tc.tile_pool(name="small", bufs=3))
-        pst = ctx.enter_context(tc.psum_pool(name="pst", bufs=4))
+        pst = ctx.enter_context(tc.psum_pool(name="pst", bufs=5))
         psc = ctx.enter_context(tc.psum_pool(name="psc", bufs=1))
         ctx.enter_context(tc.manual_schedule())
 
@@ -158,6 +159,7 @@ def tile_csocrgattention_kernel(tc, latent, alpha, grad_out, out):
         accds = {}
         negcs = {}
         tots = {}
+        haccs = {}
         tvs = {}
 
         def live(t):
@@ -281,6 +283,8 @@ def tile_csocrgattention_kernel(tc, latent, alpha, grad_out, out):
                 return
             t, h = pending[c]
             pending[c] = None
+            if c == GC:
+                return
             i = t % NT
             if i == 0:
                 cacc = psc.tile([P, CH], F32, tag="ca%d" % c, name="ca%d_%d" % (c, t))
@@ -356,13 +360,24 @@ def tile_csocrgattention_kernel(tc, latent, alpha, grad_out, out):
                     nc.vector.scalar_tensor_tensor(
                         out=h[:], in0=pbl[c][:], scalar=negcs[t][:, 0:1], in1=wch[t][c][:], op0=ALU.add, op1=ALU.mult,
                     )
+                    first = c == GC and t % NT == 0
+                    if first:
+                        hacc = work.tile([P, CH], F32, tag="hacc", bufs=2)
+                        haccs[t // NT] = hacc
                     nc.scalar.activation(
-                        out=h[:], in_=h[:], func=ACT.Copy, scale=ws[:, t : t + 1],
+                        out=haccs[t // NT][:] if first else h[:], in_=h[:], func=ACT.Copy, scale=ws[:, t : t + 1],
                         accum_out=rpart[:, NC * t + c : NC * t + c + 1],
                     )
                     pending[c] = (t, h)
+            if live(t) and t % NT > 0:
+                hacc = haccs[t // NT]
+                nc.gpsimd.tensor_tensor(out=hacc[:], in0=hacc[:], in1=pending[GC][1][:], op=ALU.add)
 
         def read_c(b):
+            gt = pst.tile([P, CH], F32, tag="tp")
+            for q in range(4):
+                nc.tensor.transpose(gt[:, P * q : P * (q + 1)], haccs[b][:, P * q : P * (q + 1)], ident[:])
+            caccs[GC] = gt
             for c in range(NC):
                 nc.vector.tensor_reduce(
                     out=cs[:, NT * b + 4 * c : NT * b + 4 * (c + 1)],

@@ -26,6 +26,7 @@ LAM = 64.0
 CEN = N - P
 TABW = 2 * N - P
 STEPS = B * NT
+LOADS = 3
 GC = 0
 
 FLOPS = 2 * B * N * N * D
@@ -123,7 +124,7 @@ def tile_csocrgattention_kernel(tc, latent, alpha, grad_out, out):
         def g_load(n):
             if n < len(groups):
                 src, b, g = groups[n][0:3]
-                xsb = stage.tile([P, 4, D], BF16, tag="xsb", bufs=2)
+                xsb = stage.tile([P, 4, D], BF16, tag="xsb", bufs=LOADS)
                 nc.sync.dma_start(out=xsb[:], in_=src[b, CH * g : CH * (g + 1), :].rearrange("(a p) d -> p a d", p=P))
                 xsbs[n] = xsb
 
@@ -159,6 +160,8 @@ def tile_csocrgattention_kernel(tc, latent, alpha, grad_out, out):
         accds = {}
         negcs = {}
         tots = {}
+        klos = {}
+        wrows = {}
         haccs = {}
         tvs = {}
 
@@ -223,7 +226,14 @@ def tile_csocrgattention_kernel(tc, latent, alpha, grad_out, out):
             accd = small.tile([P, 24], F32, tag="accd")
             accds[t] = accd
             kch[t] = [None] * c0 + [kpi[:, CH * (c - c0) : CH * (c - c0 + 1)] for c in range(c0, NC)]
-            wch[t] = [None] * NC
+            if c0 > 0:
+                klo = work.tile([P, CH * (NC - 1)], F32, tag="klo", bufs=2)
+                klos[t] = klo
+                for c in range(c0):
+                    kch[t][c] = klo[:, CH * c : CH * (c + 1)]
+            wrow = work.tile([P, N], F32, tag="w", bufs=2)
+            wrows[t] = wrow
+            wch[t] = [wrow[:, CH * c : CH * (c + 1)] for c in range(NC)]
             tvs[t] = [(c, m if c == c0 else 0) for c in range(c0, NC)]
 
         def n_tk(t):
@@ -241,20 +251,22 @@ def tile_csocrgattention_kernel(tc, latent, alpha, grad_out, out):
                 j = 4 * c + q
                 off = P * i - CH * c
                 nc.tensor.transpose(kt[:, P * q : P * (q + 1)], kp[j][:, off : off + P], ident[:])
-            if c < c0:
-                klo = work.tile([P, CH], F32, tag="klo", bufs=6)
-                dst = klo[:]
-                kch[t][c] = dst
-            else:
-                dst = kp[i][:, 0 : P * m]
+            dst = kch[t][c] if c < c0 else kp[i][:, 0 : P * m]
             nc.scalar.activation(out=dst, in_=kt[:, 0 : P * nb], func=ACT.Copy, accum_out=accds[t][:, 16 + c : 17 + c])
-            one_w(t, c)
 
-        def one_w(t, c):
-            x0 = CEN - P * (t % NT)
-            w = work.tile([P, CH], F32, tag="w", bufs=8)
-            nc.gpsimd.tensor_tensor(out=w[:], in0=kch[t][c], in1=tab[:, x0 + CH * c : x0 + CH * (c + 1)], op=ALU.mult)
-            wch[t][c] = w
+        def w_right(t):
+            if live(t):
+                i = t % NT
+                c0 = i // 4
+                x0 = CEN - P * i
+                nc.gpsimd.tensor_tensor(out=wrows[t][:, CH * c0 : N], in0=kp[i][:], in1=tab[:, x0 + CH * c0 : x0 + N], op=ALU.mult)
+
+        def w_left(t):
+            if live(t) and (t % NT) // 4 > 0:
+                i = t % NT
+                c0 = i // 4
+                x0 = CEN - P * i
+                nc.gpsimd.tensor_tensor(out=wrows[t][:, 0 : CH * c0], in0=klos[t][:, 0 : CH * c0], in1=tab[:, x0 : x0 + CH * c0], op=ALU.mult)
 
         def small_s(t):
             if live(t):
@@ -316,8 +328,6 @@ def tile_csocrgattention_kernel(tc, latent, alpha, grad_out, out):
                     in1=urows[t][:, uo : uo + nw], op0=ALU.mult, op1=ALU.mult,
                     accum_out=accds[t][:, 12 + c : 13 + c],
                 )
-                if lo == 0:
-                    one_w(t, c)
             flush_ht(3)
 
         def stage_p(t, c):
@@ -358,7 +368,7 @@ def tile_csocrgattention_kernel(tc, latent, alpha, grad_out, out):
                 if live(t):
                     h = work.tile([P, CH], F32, tag="h", bufs=6)
                     nc.vector.scalar_tensor_tensor(
-                        out=h[:], in0=pbl[c][:], scalar=negcs[t][:, 0:1], in1=wch[t][c][:], op0=ALU.add, op1=ALU.mult,
+                        out=h[:], in0=pbl[c][:], scalar=negcs[t][:, 0:1], in1=wch[t][c], op0=ALU.add, op1=ALU.mult,
                     )
                     first = c == GC and t % NT == 0
                     if first:
@@ -378,23 +388,25 @@ def tile_csocrgattention_kernel(tc, latent, alpha, grad_out, out):
             for q in range(4):
                 nc.tensor.transpose(gt[:, P * q : P * (q + 1)], haccs[b][:, P * q : P * (q + 1)], ident[:])
             caccs[GC] = gt
-            for c in range(NC):
+            for c in [c for c in range(NC) if c != GC] + [GC]:
                 nc.vector.tensor_reduce(
                     out=cs[:, NT * b + 4 * c : NT * b + 4 * (c + 1)],
                     in_=caccs[c][:].rearrange("p (q r) -> p q r", q=4), axis=AX.X, op=ALU.add,
                 )
 
-        for n in range(2):
+        for n in range(LOADS):
             g_load(n)
         stage_u(0)
         stage_u_rest(0)
         for n in range(HEAD):
             g_tr(n, True)
-            g_load(n + 2)
+            g_load(n + LOADS)
             if n > 0:
                 g_q(n - 1)
         g_q(HEAD - 1)
         pool_ud(0)
+        fin = d0
+        nc.vector.memset(fin[:], 0.0)
         for s in range(-2, STEPS - 1):
             if s == NT:
                 read_c(0)
@@ -405,8 +417,13 @@ def tile_csocrgattention_kernel(tc, latent, alpha, grad_out, out):
             alloc_step(s + 2)
             pool_ud(s + 3)
             k_phase(s + 2)
-            for c in range(n_tk(s + 2)):
+            ntk = n_tk(s + 2)
+            if ntk > 0 and (s + 2) % 4 > 0:
+                tk_unit(s + 2, ntk - 1)
+            w_right(s + 2)
+            for c in range(ntk - (1 if (s + 2) % 4 > 0 else 0)):
                 tk_unit(s + 2, c)
+            w_left(s + 2)
             small_s(s + 2)
             n = HEAD + s + 2
             if HEAD < n <= len(groups):
@@ -414,18 +431,16 @@ def tile_csocrgattention_kernel(tc, latent, alpha, grad_out, out):
             h_phase(s + 1, s + 2)
             if n < len(groups):
                 g_tr(n, False)
-                g_load(n + 2)
+                g_load(n + LOADS)
         for c in range(NC):
             flush_ht(c)
         read_c(1)
 
         rs = const.tile([P, STEPS], F32)
         nc.vector.tensor_reduce(out=rs[:], in_=rpart[:].rearrange("p (t c) -> p t c", c=NC), axis=AX.X, op=ALU.add)
-        fin = const.tile([P, P], F32)
-        nc.vector.memset(fin[:], 0.0)
         nc.vector.tensor_tensor(out=fin[:, 0:STEPS], in0=rs[:], in1=cs[:], op=ALU.add)
         fps = pst.tile([P, CH], F32, tag="tp")
         nc.tensor.transpose(fps[:, 0:P], fin[:], ident[:])
-        osb = const.tile([P, P], F32)
+        osb = nd0
         nc.vector.tensor_scalar(out=osb[:], in0=fps[:, 0:P], scalar1=0.5, scalar2=None, op0=ALU.mult)
         nc.sync.dma_start(out=out.rearrange("b (t p) -> (b t) p", p=P), in_=osb[0:STEPS, :])

@@ -124,7 +124,10 @@ def tile_csocrgattention_kernel(tc, latent, alpha, grad_out, out):
         def g_load(n):
             if n < len(groups):
                 src, b, g = groups[n][0:3]
-                xsb = stage.tile([P, 4, D], BF16, tag="xsb", bufs=LOADS)
+                if LOADS <= n < HEAD:
+                    xsb = work.tile([P, 4, D], BF16, tag="w", bufs=2)
+                else:
+                    xsb = stage.tile([P, 4, D], BF16, tag="xsb", bufs=LOADS)
                 nc.sync.dma_start(out=xsb[:], in_=src[b, CH * g : CH * (g + 1), :].rearrange("(a p) d -> p a d", p=P))
                 xsbs[n] = xsb
 
@@ -214,6 +217,8 @@ def tile_csocrgattention_kernel(tc, latent, alpha, grad_out, out):
                 else:
                     srcb = ulcs[t][:, P * (j - i - 1) : P * (j - i)]
                 nc.tensor.transpose(vt[:, P * (q - lo) : P * (q - lo + 1)], srcb, ident[:])
+            for q in range(lo):
+                nc.tensor.transpose(vt[:, P * (4 - lo + q) : P * (5 - lo + q)], kp[4 * c + q][:, P * i - CH * c : P * (i + 1) - CH * c], ident[:])
             return vt
 
         def alloc_step(t):
@@ -328,6 +333,10 @@ def tile_csocrgattention_kernel(tc, latent, alpha, grad_out, out):
                     in1=urows[t][:, uo : uo + nw], op0=ALU.mult, op1=ALU.mult,
                     accum_out=accds[t][:, 12 + c : 13 + c],
                 )
+                if lo > 0:
+                    nc.scalar.activation(
+                        out=kp[i][:, 0 : P * lo], in_=bank[:, nw:CH], func=ACT.Copy, accum_out=accds[t][:, 16 + c : 17 + c]
+                    )
             flush_ht(3)
 
         def stage_p(t, c):
@@ -394,13 +403,14 @@ def tile_csocrgattention_kernel(tc, latent, alpha, grad_out, out):
                     in_=caccs[c][:].rearrange("p (q r) -> p q r", q=4), axis=AX.X, op=ALU.add,
                 )
 
-        for n in range(LOADS):
+        for n in range(HEAD):
             g_load(n)
         stage_u(0)
         stage_u_rest(0)
         for n in range(HEAD):
             g_tr(n, True)
-            g_load(n + LOADS)
+            if n < LOADS:
+                g_load(n + HEAD)
             if n > 0:
                 g_q(n - 1)
         g_q(HEAD - 1)
@@ -418,8 +428,6 @@ def tile_csocrgattention_kernel(tc, latent, alpha, grad_out, out):
             pool_ud(s + 3)
             k_phase(s + 2)
             ntk = n_tk(s + 2)
-            if ntk > 0 and (s + 2) % 4 > 0:
-                tk_unit(s + 2, ntk - 1)
             w_right(s + 2)
             for c in range(ntk - (1 if (s + 2) % 4 > 0 else 0)):
                 tk_unit(s + 2, c)

@@ -27,6 +27,7 @@ CEN = N - P
 TABW = 2 * N - P
 STEPS = B * NT
 LOADS = 3
+FAR = 2
 GC = 0
 
 FLOPS = 2 * B * N * N * D
@@ -168,6 +169,11 @@ def tile_csocrgattention_kernel(tc, latent, alpha, grad_out, out):
         haccs = {}
         tvs = {}
 
+        dgs = {}
+
+        def far(i, c):
+            return c >= i // 4 + FAR
+
         def live(t):
             return 0 <= t < STEPS
 
@@ -193,11 +199,16 @@ def tile_csocrgattention_kernel(tc, latent, alpha, grad_out, out):
                 for j in range(i + 1, NT):
                     blk = NT - 1 - j + i
                     nc.scalar.activation(
-                        out=ulc[:, P * (j - i - 1) : P * (j - i)], in_=tab[:, P * blk : P * (blk + 1)], func=ACT.Exp,
+                        out=ulc[:, P * (j - i - 1) : P * (j - i)], in_=tab[:, P * blk : P * (blk + 1)],
+                        func=ACT.Identity if far(i, j // 4) else ACT.Exp,
                         scale=nega[:, b * NT + j : b * NT + j + 1], bias=bl[:, j : j + 1],
                     )
                 ulcs[t] = ulc
-                wd = N - P * (i + 1)
+                wd = min(N, CH * (i // 4 + FAR)) - P * (i + 1)
+                if far(i, NC - 1):
+                    dg = upool.tile([P, P], F32, tag="dg")
+                    nc.scalar.activation(out=dg[:], in_=ident[:], func=ACT.Copy, scale=sc)
+                    dgs[t] = dg
                 nc.scalar.activation(
                     out=urow[:, P : P + wd], in_=tab[:, R0 : R0 + wd], func=ACT.Exp, scale=sc, bias=br[:, i : i + 1]
                 )
@@ -210,6 +221,16 @@ def tile_csocrgattention_kernel(tc, latent, alpha, grad_out, out):
             i = t % NT
             c, lo = unit
             vt = pst.tile([P, CH], F32, tag="tp")
+            if far(i, c):
+                x0 = CEN - P * i
+                nc.tensor.matmul(out=vt[:], lhsT=dgs[t][:], rhs=tab[:, x0 + CH * c : x0 + CH * (c + 1)], start=True, stop=False)
+                for q in range(4):
+                    j = 4 * c + q
+                    nc.tensor.matmul(
+                        out=vt[:, P * q : P * (q + 1)], lhsT=ulcs[t][:, P * (j - i - 1) : P * (j - i)], rhs=ident[:],
+                        is_transpose=True, start=False, stop=(q == 3),
+                    )
+                return vt
             for q in range(lo, 4):
                 j = 4 * c + q
                 if j == i:
@@ -328,6 +349,12 @@ def tile_csocrgattention_kernel(tc, latent, alpha, grad_out, out):
                 nw = P * (4 - lo)
                 uo = P * (4 * c + lo - i)
                 base = CH * (c - c0)
+                if far(i, c):
+                    nc.scalar.activation(
+                        out=kp[i][:, base : base + CH], in_=bank[:], func=ACT.Exp, bias=br[:, i : i + 1],
+                        accum_out=accds[t][:, 12 + c : 13 + c],
+                    )
+                    continue
                 nc.vector.scalar_tensor_tensor(
                     out=kp[i][:, base + P * lo : base + CH], in0=bank[:, 0:nw], scalar=1.0,
                     in1=urows[t][:, uo : uo + nw], op0=ALU.mult, op1=ALU.mult,
@@ -375,7 +402,7 @@ def tile_csocrgattention_kernel(tc, latent, alpha, grad_out, out):
                 pbl = [stage_p(t, c) for c in range(NC)]
             for c in range(NC):
                 if live(t):
-                    h = work.tile([P, CH], F32, tag="h", bufs=6)
+                    h = work.tile([P, CH], F32, tag="h", bufs=5)
                     nc.vector.scalar_tensor_tensor(
                         out=h[:], in0=pbl[c][:], scalar=negcs[t][:, 0:1], in1=wch[t][c], op0=ALU.add, op1=ALU.mult,
                     )

@@ -27,7 +27,15 @@ CEN = N - P
 TABW = 2 * N - P
 STEPS = B * NT
 LOADS = 3
-FAR = 2
+GV = 1
+DG = 6
+UL = 8
+UR = 4
+LEAD = 9
+Q0 = 4
+LV = ((0, 0, 0, 1), (0, 0, 0, 1))
+DP = ((0, 0, 0, 0), (0, 0, 0, 0))
+NEAR = 1
 GC = 0
 
 FLOPS = 2 * B * N * N * D
@@ -91,6 +99,8 @@ def tile_csocrgattention_kernel(tc, latent, alpha, grad_out, out):
         nc.scalar.activation(out=tab[:, R0:TABW], in_=tab[:, R0:TABW], func=ACT.Ln)
         sqt = const.tile([P, P], F32)
         nc.scalar.activation(out=sqt[:], in_=rd[:], func=ACT.Exp, scale=-0.5 / LAM)
+        ct = const.tile([P, P], F32)
+        nc.vector.tensor_scalar(out=ct[:], in0=d0[:], scalar1=0.0, scalar2=2.0 / LAM, op0=ALU.min, op1=ALU.mult)
 
         br = const.tile([P, NT], F32)
         nc.vector.tensor_scalar(out=br[:], in0=rowi[:], scalar1=1.0 / LAM, scalar2=None, op0=ALU.mult)
@@ -144,7 +154,7 @@ def tile_csocrgattention_kernel(tc, latent, alpha, grad_out, out):
                     for u in range(2):
                         nc.tensor.transpose(xt[:, a, u, :], words[:, P * u : P * (u + 1)], ident[:])
                 sview = xt[:].rearrange("p a u r -> p a r u")
-                if on_vector:
+                if on_vector > hf:
                     nc.vector.tensor_copy(out=gview[:, 2 * hf : 2 * hf + 2], in_=sview)
                 else:
                     nc.scalar.copy(out=gview[:, 2 * hf : 2 * hf + 2], in_=sview)
@@ -157,7 +167,6 @@ def tile_csocrgattention_kernel(tc, latent, alpha, grad_out, out):
 
         kp = {}
         urows = {}
-        ud0s = {}
         ulcs = {}
         kch = {}
         wch = {}
@@ -171,73 +180,92 @@ def tile_csocrgattention_kernel(tc, latent, alpha, grad_out, out):
 
         dgs = {}
 
-        def far(i, c):
-            return c >= i // 4 + FAR
+        def byvec(t, c):
+            b, i = divmod(t, NT)
+            d = c - i // 4
+            return 0 < d <= NEAR or (d == 0 and not DP[b][i // 4])
 
         def live(t):
             return 0 <= t < STEPS
 
-        def stage_u(t):
-            if not live(t):
-                return
-            b, i = divmod(t, NT)
-            urow = upool.tile([P, N], F32, tag="urow")
-            ud0 = upool.tile([P, P], F32, tag="ud0")
-            sc = nega[:, t : t + 1]
-            nc.scalar.activation(out=ud0[:], in_=tab[:, CEN:R0], func=ACT.Exp, scale=sc)
-            urows[t] = urow
-            ud0s[t] = ud0
+        pieces = []
+        for t in range(STEPS):
+            for c in range((t % NT) // 4, NC):
+                pieces.append((t, c, 0))
+                if byvec(t, c):
+                    pieces.append((t, c, 1))
+        made = [0]
+        used = [0]
 
-        def stage_u_rest(t):
-            if not live(t):
-                return
+        def make_u():
+            if made[0] == len(pieces):
+                return False
+            t, c, half = pieces[made[0]]
             b, i = divmod(t, NT)
-            urow = urows[t]
-            sc = nega[:, t : t + 1]
-            if i < NT - 1:
-                ulc = upool.tile([P, N - P], F32, tag="ulc")
-                for j in range(i + 1, NT):
+            if half == 0:
+                if not byvec(t, c) and t not in dgs:
+                    dg = upool.tile([P, P], F32, tag="dg", bufs=DG)
+                    nc.scalar.activation(out=dg[:], in_=ident[:], func=ACT.Copy, scale=nega[:, t : t + 1])
+                    dgs[t] = dg
+                ulc = upool.tile([P, CH], F32, tag="ulc", bufs=UL)
+                for j in range(max(i + byvec(t, c), 4 * c), 4 * c + 4):
                     blk = NT - 1 - j + i
                     nc.scalar.activation(
-                        out=ulc[:, P * (j - i - 1) : P * (j - i)], in_=tab[:, P * blk : P * (blk + 1)],
-                        func=ACT.Identity if far(i, j // 4) else ACT.Exp,
+                        out=ulc[:, P * (j - 4 * c) : P * (j - 4 * c + 1)], in_=tab[:, P * blk : P * (blk + 1)],
+                        func=ACT.Exp if byvec(t, c) else ACT.Identity,
                         scale=nega[:, b * NT + j : b * NT + j + 1], bias=bl[:, j : j + 1],
                     )
-                ulcs[t] = ulc
-                wd = min(N, CH * (i // 4 + FAR)) - P * (i + 1)
-                if far(i, NC - 1):
-                    dg = upool.tile([P, P], F32, tag="dg")
-                    nc.scalar.activation(out=dg[:], in_=ident[:], func=ACT.Copy, scale=sc)
-                    dgs[t] = dg
-                nc.scalar.activation(
-                    out=urow[:, P : P + wd], in_=tab[:, R0 : R0 + wd], func=ACT.Exp, scale=sc, bias=br[:, i : i + 1]
-                )
+                ulcs[(t, c)] = ulc
+            else:
+                urow = upool.tile([P, CH], F32, tag="urow", bufs=UR)
+                x0 = CEN - P * i + CH * c
+                lo = 0
+                if c == i // 4:
+                    lo = i % 4 + 1
+                    ud0 = upool.tile([P, P], F32, tag="ud0", bufs=2)
+                    nc.scalar.activation(out=ud0[:], in_=tab[:, CEN:R0], func=ACT.Exp, scale=nega[:, t : t + 1])
+                    nc.gpsimd.tensor_tensor(out=urow[:, P * (lo - 1) : P * lo], in0=ud0[:], in1=sqt[:], op=ALU.mult)
+                if lo < 4:
+                    nc.scalar.activation(
+                        out=urow[:, P * lo : CH], in_=tab[:, x0 + P * lo : x0 + CH], func=ACT.Exp,
+                        scale=nega[:, t : t + 1], bias=br[:, i : i + 1],
+                    )
+                urows[(t, c)] = urow
+            made[0] += 1
+            return True
 
-        def pool_ud(t):
-            if live(t):
-                nc.gpsimd.tensor_tensor(out=urows[t][:, 0:P], in0=ud0s[t][:], in1=sqt[:], op=ALU.mult)
+        def can_make():
+            return made[0] < len(pieces) and made[0] - used[0] < LEAD
+
+        def make_some(n):
+            for q in range(n):
+                if can_make():
+                    make_u()
+
+        def make_until(t):
+            while made[0] < len(pieces) and pieces[made[0]][0] <= t:
+                make_u()
 
         def fill_tv(t, unit):
             i = t % NT
             c, lo = unit
             vt = pst.tile([P, CH], F32, tag="tp")
-            if far(i, c):
-                x0 = CEN - P * i
-                nc.tensor.matmul(out=vt[:], lhsT=dgs[t][:], rhs=tab[:, x0 + CH * c : x0 + CH * (c + 1)], start=True, stop=False)
-                for q in range(4):
-                    j = 4 * c + q
-                    nc.tensor.matmul(
-                        out=vt[:, P * q : P * (q + 1)], lhsT=ulcs[t][:, P * (j - i - 1) : P * (j - i)], rhs=ident[:],
-                        is_transpose=True, start=False, stop=(q == 3),
-                    )
-                return vt
+            nw = P * (4 - lo)
+            used[0] += 2 if byvec(t, c) else 1
+            if not byvec(t, c):
+                x0 = CEN - P * i + CH * c + P * lo
+                nc.tensor.matmul(out=vt[:, 0:nw], lhsT=dgs[t][:], rhs=tab[:, x0 : x0 + nw], start=True, stop=False)
             for q in range(lo, 4):
                 j = 4 * c + q
-                if j == i:
-                    srcb = urows[t][:, 0:P]
+                o = vt[:, P * (q - lo) : P * (q - lo + 1)]
+                if byvec(t, c):
+                    srcb = urows[(t, c)][:, P * q : P * (q + 1)] if j == i else ulcs[(t, c)][:, P * q : P * (q + 1)]
+                    nc.tensor.transpose(o, srcb, ident[:])
                 else:
-                    srcb = ulcs[t][:, P * (j - i - 1) : P * (j - i)]
-                nc.tensor.transpose(vt[:, P * (q - lo) : P * (q - lo + 1)], srcb, ident[:])
+                    srcb = ulcs[(t, c)][:, P * q : P * (q + 1)]
+                    nc.tensor.matmul(out=o, lhsT=srcb, rhs=ident[:], is_transpose=True, start=False, stop=(q == 3 and j != i))
+                    if j == i:
+                        nc.tensor.matmul(out=o, lhsT=ct[:], rhs=ident[:], is_transpose=True, start=False, stop=(q == 3))
             for q in range(lo):
                 nc.tensor.transpose(vt[:, P * (4 - lo + q) : P * (5 - lo + q)], kp[4 * c + q][:, P * i - CH * c : P * (i + 1) - CH * c], ident[:])
             return vt
@@ -278,7 +306,12 @@ def tile_csocrgattention_kernel(tc, latent, alpha, grad_out, out):
                 off = P * i - CH * c
                 nc.tensor.transpose(kt[:, P * q : P * (q + 1)], kp[j][:, off : off + P], ident[:])
             dst = kch[t][c] if c < c0 else kp[i][:, 0 : P * m]
-            nc.scalar.activation(out=dst, in_=kt[:, 0 : P * nb], func=ACT.Copy, accum_out=accds[t][:, 16 + c : 17 + c])
+            if c < LV[t // NT][c0]:
+                nc.vector.tensor_scalar(
+                    out=dst, in0=kt[:], scalar1=1.0, scalar2=None, op0=ALU.mult, op1=ALU.add, accum_out=accds[t][:, 16 + c : 17 + c]
+                )
+            else:
+                nc.scalar.activation(out=dst, in_=kt[:, 0 : P * nb], func=ACT.Copy, accum_out=accds[t][:, 16 + c : 17 + c])
 
         def w_right(t):
             if live(t):
@@ -288,11 +321,12 @@ def tile_csocrgattention_kernel(tc, latent, alpha, grad_out, out):
                 nc.gpsimd.tensor_tensor(out=wrows[t][:, CH * c0 : N], in0=kp[i][:], in1=tab[:, x0 + CH * c0 : x0 + N], op=ALU.mult)
 
         def w_left(t):
-            if live(t) and (t % NT) // 4 > 0:
-                i = t % NT
-                c0 = i // 4
+            i = t % NT
+            c0 = i // 4
+            n = CH * c0
+            if live(t) and n > 0:
                 x0 = CEN - P * i
-                nc.gpsimd.tensor_tensor(out=wrows[t][:, 0 : CH * c0], in0=klos[t][:, 0 : CH * c0], in1=tab[:, x0 : x0 + CH * c0], op=ALU.mult)
+                nc.gpsimd.tensor_tensor(out=wrows[t][:, 0:n], in0=klos[t][:, 0:n], in1=tab[:, x0 : x0 + n], op=ALU.mult)
 
         def small_s(t):
             if live(t):
@@ -347,19 +381,18 @@ def tile_csocrgattention_kernel(tc, latent, alpha, grad_out, out):
                 if idx < 2:
                     flush_ht(2 + idx)
                 nw = P * (4 - lo)
-                uo = P * (4 * c + lo - i)
                 base = CH * (c - c0)
-                if far(i, c):
-                    nc.scalar.activation(
-                        out=kp[i][:, base : base + CH], in_=bank[:], func=ACT.Exp, bias=br[:, i : i + 1],
+                if byvec(t, c):
+                    nc.vector.scalar_tensor_tensor(
+                        out=kp[i][:, base + P * lo : base + CH], in0=bank[:, 0:nw], scalar=1.0,
+                        in1=urows[(t, c)][:, P * lo : CH], op0=ALU.mult, op1=ALU.mult,
                         accum_out=accds[t][:, 12 + c : 13 + c],
                     )
-                    continue
-                nc.vector.scalar_tensor_tensor(
-                    out=kp[i][:, base + P * lo : base + CH], in0=bank[:, 0:nw], scalar=1.0,
-                    in1=urows[t][:, uo : uo + nw], op0=ALU.mult, op1=ALU.mult,
-                    accum_out=accds[t][:, 12 + c : 13 + c],
-                )
+                else:
+                    nc.scalar.activation(
+                        out=kp[i][:, base + P * lo : base + CH], in_=bank[:, 0:nw], func=ACT.Exp, bias=br[:, i : i + 1],
+                        accum_out=accds[t][:, 12 + c : 13 + c],
+                    )
                 if lo > 0:
                     nc.scalar.activation(
                         out=kp[i][:, 0 : P * lo], in_=bank[:, nw:CH], func=ACT.Copy, accum_out=accds[t][:, 16 + c : 17 + c]
@@ -432,27 +465,24 @@ def tile_csocrgattention_kernel(tc, latent, alpha, grad_out, out):
 
         for n in range(HEAD):
             g_load(n)
-        stage_u(0)
-        stage_u_rest(0)
+        make_until(0)
         for n in range(HEAD):
-            g_tr(n, True)
+            g_tr(n, 2)
             if n < LOADS:
                 g_load(n + HEAD)
             if n > 0:
                 g_q(n - 1)
         g_q(HEAD - 1)
-        pool_ud(0)
         fin = d0
         nc.vector.memset(fin[:], 0.0)
         for s in range(-2, STEPS - 1):
             if s == NT:
                 read_c(0)
-            stage_u(s + 3)
-            stage_u_rest(s + 3)
+            make_until(s + 2)
+            make_some(Q0)
             x_phase(s + 1)
             small_c(s + 1)
             alloc_step(s + 2)
-            pool_ud(s + 3)
             k_phase(s + 2)
             ntk = n_tk(s + 2)
             w_right(s + 2)
@@ -465,7 +495,7 @@ def tile_csocrgattention_kernel(tc, latent, alpha, grad_out, out):
                 g_q(n - 1)
             h_phase(s + 1, s + 2)
             if n < len(groups):
-                g_tr(n, False)
+                g_tr(n, GV)
                 g_load(n + LOADS)
         for c in range(NC):
             flush_ht(c)

@@ -33,6 +33,7 @@ UL = 8
 UR = 4
 LEAD = 9
 Q0 = 4
+HSPLIT, HK = 3, 4
 LV = ((0, 0, 0, 1), (0, 0, 0, 1))
 DP = ((0, 0, 0, 0), (0, 0, 0, 0))
 NEAR = 1
@@ -55,16 +56,12 @@ def tile_csocrgattention_kernel(tc, latent, alpha, grad_out, out):
         psc = ctx.enter_context(tc.psum_pool(name="psc", bufs=1))
         ctx.enter_context(tc.manual_schedule())
 
-        ident = const.tile([P, P], F32)
-        make_identity(nc, ident[:])
         d0i = const.tile([P, P], I32)
         nc.gpsimd.iota(d0i[:], pattern=[[-1, P]], base=0, channel_multiplier=1)
         rowi = const.tile([P, NT], I32)
         nc.gpsimd.iota(rowi[:], pattern=[[P, NT]], base=-(N // 2), channel_multiplier=1)
-
-        abf = const.tile([P, P], BF16)
-        nc.vector.memset(abf[:], 0.0)
-        nc.sync.dma_start(out=abf[0 : B * NT, :], in_=alpha.rearrange("b (t p) -> (b t) p", p=P))
+        ident = const.tile([P, P], F32)
+        make_identity(nc, ident[:])
 
         d0 = const.tile([P, P], F32)
         nc.vector.tensor_copy(out=d0[:], in_=d0i[:])
@@ -72,47 +69,33 @@ def tile_csocrgattention_kernel(tc, latent, alpha, grad_out, out):
         nc.vector.tensor_scalar(out=nd0[:], in0=d0[:], scalar1=-1.0, scalar2=None, op0=ALU.mult)
         rd = const.tile([P, P], F32)
         nc.vector.tensor_tensor(out=rd[:], in0=d0[:], in1=nd0[:], op=ALU.max)
-        nc.vector.tensor_scalar(out=rd[:], in0=rd[:], scalar1=EPS, scalar2=None, op0=ALU.add)
-
-        tab = const.tile([P, TABW], F32)
-        nc.vector.tensor_scalar(out=tab[:, CEN - P : CEN], in0=d0[:], scalar1=P + EPS, scalar2=None, op0=ALU.add)
-        filled = P
-        while filled < CEN:
-            n = min(filled, CEN - filled)
-            nc.vector.tensor_scalar(
-                out=tab[:, CEN - filled - n : CEN - filled], in0=tab[:, CEN - n : CEN],
-                scalar1=float(filled), scalar2=None, op0=ALU.add,
-            )
-            filled += n
-        R0 = CEN + P
-        nc.vector.tensor_scalar(out=tab[:, R0 : R0 + P], in0=nd0[:], scalar1=P + EPS, scalar2=None, op0=ALU.add)
-        filled = P
-        while filled < CEN:
-            n = min(filled, CEN - filled)
-            nc.vector.tensor_scalar(
-                out=tab[:, R0 + filled : R0 + filled + n], in0=tab[:, R0 : R0 + n],
-                scalar1=float(filled), scalar2=None, op0=ALU.add,
-            )
-            filled += n
-        nc.scalar.activation(out=tab[:, CEN:R0], in_=rd[:], func=ACT.Ln)
-        nc.scalar.activation(out=tab[:, 0:CEN], in_=tab[:, 0:CEN], func=ACT.Ln)
-        nc.scalar.activation(out=tab[:, R0:TABW], in_=tab[:, R0:TABW], func=ACT.Ln)
-        sqt = const.tile([P, P], F32)
-        nc.scalar.activation(out=sqt[:], in_=rd[:], func=ACT.Exp, scale=-0.5 / LAM)
         ct = const.tile([P, P], F32)
         nc.vector.tensor_scalar(out=ct[:], in0=d0[:], scalar1=0.0, scalar2=2.0 / LAM, op0=ALU.min, op1=ALU.mult)
-
         br = const.tile([P, NT], F32)
         nc.vector.tensor_scalar(out=br[:], in0=rowi[:], scalar1=1.0 / LAM, scalar2=None, op0=ALU.mult)
         bl = const.tile([P, NT], F32)
         nc.vector.tensor_scalar(out=bl[:], in0=rowi[:], scalar1=-1.0 / LAM, scalar2=-EPS / LAM, op0=ALU.mult, op1=ALU.add)
 
+        tab = const.tile([P, TABW], F32)
+        R0 = CEN + P
+        for k in range(1, NT):
+            nc.scalar.activation(out=tab[:, CEN - P * k : R0 - P * k], in_=d0[:], func=ACT.Ln, bias=P * k + EPS)
+        nc.scalar.activation(out=tab[:, CEN:R0], in_=rd[:], func=ACT.Ln, bias=EPS)
+        for k in range(1, NT):
+            nc.scalar.activation(out=tab[:, CEN + P * k : R0 + P * k], in_=nd0[:], func=ACT.Ln, bias=P * k + EPS)
+        sqt = const.tile([P, P], F32)
+        nc.scalar.activation(out=sqt[:], in_=rd[:], func=ACT.Exp, scale=-0.5 / LAM, bias=-0.5 * EPS / LAM)
+
+        abf = const.tile([P, P], BF16)
+        nc.vector.memset(abf[:], 0.0)
         af = const.tile([P, P], F32)
-        nc.vector.tensor_copy(out=af[:], in_=abf[:])
-        aps = pst.tile([P, CH], F32, tag="tp")
-        nc.tensor.transpose(aps[:, 0:P], af[:], ident[:])
         nega = const.tile([P, STEPS], F32)
-        nc.vector.tensor_scalar(out=nega[:], in0=aps[:, 0:STEPS], scalar1=-0.5, scalar2=None, op0=ALU.mult)
+
+        def make_nega():
+            nc.vector.tensor_copy(out=af[:], in_=abf[:])
+            aps = pst.tile([P, CH], F32, tag="tp")
+            nc.tensor.transpose(aps[:, 0:P], af[:], ident[:])
+            nc.vector.tensor_scalar(out=nega[:], in0=aps[:, 0:STEPS], scalar1=-0.5, scalar2=None, op0=ALU.mult)
 
         ws = const.tile([P, STEPS], F32)
         rpart = const.tile([P, STEPS * NC], F32)
@@ -136,7 +119,7 @@ def tile_csocrgattention_kernel(tc, latent, alpha, grad_out, out):
             if n < len(groups):
                 src, b, g = groups[n][0:3]
                 if LOADS <= n < HEAD:
-                    xsb = work.tile([P, 4, D], BF16, tag="w", bufs=2)
+                    xsb = kpool.tile([P, 4, D], BF16, tag="kp%d" % (8 + n - LOADS), name="xh%d" % n)
                 else:
                     xsb = stage.tile([P, 4, D], BF16, tag="xsb", bufs=LOADS)
                 nc.sync.dma_start(out=xsb[:], in_=src[b, CH * g : CH * (g + 1), :].rearrange("(a p) d -> p a d", p=P))
@@ -463,19 +446,7 @@ def tile_csocrgattention_kernel(tc, latent, alpha, grad_out, out):
                     in_=caccs[c][:].rearrange("p (q r) -> p q r", q=4), axis=AX.X, op=ALU.add,
                 )
 
-        for n in range(HEAD):
-            g_load(n)
-        make_until(0)
-        for n in range(HEAD):
-            g_tr(n, 2)
-            if n < LOADS:
-                g_load(n + HEAD)
-            if n > 0:
-                g_q(n - 1)
-        g_q(HEAD - 1)
-        fin = d0
-        nc.vector.memset(fin[:], 0.0)
-        for s in range(-2, STEPS - 1):
+        def step(s):
             if s == NT:
                 read_c(0)
             make_until(s + 2)
@@ -494,9 +465,32 @@ def tile_csocrgattention_kernel(tc, latent, alpha, grad_out, out):
             if HEAD < n <= len(groups):
                 g_q(n - 1)
             h_phase(s + 1, s + 2)
-            if n < len(groups):
+            if HEAD < n + 1 and n < len(groups) and s > -2:
                 g_tr(n, GV)
                 g_load(n + LOADS)
+
+        g_load(0)
+        nc.sync.dma_start(out=abf[0 : B * NT, :], in_=alpha.rearrange("b (t p) -> (b t) p", p=P))
+        for n in range(1, HEAD):
+            g_load(n)
+        for n in range(HEAD):
+            g_tr(n, 2 if n < HSPLIT else 1)
+            if n < LOADS:
+                g_load(n + HEAD)
+            if n == 0:
+                make_nega()
+                make_until(0)
+            if n > 0:
+                g_q(n - 1)
+            if n == HK:
+                step(-2)
+        g_q(HEAD - 1)
+        g_tr(HEAD, GV)
+        g_load(HEAD + LOADS)
+        fin = d0
+        nc.vector.memset(fin[:], 0.0)
+        for s in range(-1, STEPS - 1):
+            step(s)
         for c in range(NC):
             flush_ht(c)
         read_c(1)

@@ -33,10 +33,18 @@ UL = 8
 UR = 4
 LEAD = 9
 Q0 = 4
+EARLYMM = False
+FX, FK, FB = (0, 1), (2, 3), ()
+HB = 8
+GPOS = 2
+DEEP = 0
+QPOS = 2
+WSPLIT = 0
+TURNS = {n - 7: n for n in range(6, 16)}
 HSPLIT, HK = 3, 4
 LV = ((0, 0, 0, 1), (0, 0, 0, 1))
 DP = ((0, 0, 0, 0), (0, 0, 0, 0))
-NEAR = 1
+NV = ((1, 1, 1, 1), (1, 1, 1, 1))
 GC = 0
 
 FLOPS = 2 * B * N * N * D
@@ -166,7 +174,7 @@ def tile_csocrgattention_kernel(tc, latent, alpha, grad_out, out):
         def byvec(t, c):
             b, i = divmod(t, NT)
             d = c - i // 4
-            return 0 < d <= NEAR or (d == 0 and not DP[b][i // 4])
+            return 0 < d <= NV[b][i // 4] or (d == 0 and not DP[b][i // 4])
 
         def live(t):
             return 0 <= t < STEPS
@@ -229,15 +237,23 @@ def tile_csocrgattention_kernel(tc, latent, alpha, grad_out, out):
             while made[0] < len(pieces) and pieces[made[0]][0] <= t:
                 make_u()
 
-        def fill_tv(t, unit):
+        def open_tv(t, unit):
             i = t % NT
             c, lo = unit
-            vt = pst.tile([P, CH], F32, tag="tp")
             nw = P * (4 - lo)
+            x0 = CEN - P * i + CH * c + P * lo
+            vt = pst.tile([P, CH], F32, tag="tp")
+            nc.tensor.matmul(out=vt[:, 0:nw], lhsT=dgs[t][:], rhs=tab[:, x0 : x0 + nw], start=True, stop=False)
+            return vt
+
+        def fill_tv(t, unit, vt=None):
+            i = t % NT
+            c, lo = unit
+            if vt is None and byvec(t, c):
+                vt = pst.tile([P, CH], F32, tag="tp")
+            elif vt is None:
+                vt = open_tv(t, unit)
             used[0] += 2 if byvec(t, c) else 1
-            if not byvec(t, c):
-                x0 = CEN - P * i + CH * c + P * lo
-                nc.tensor.matmul(out=vt[:, 0:nw], lhsT=dgs[t][:], rhs=tab[:, x0 : x0 + nw], start=True, stop=False)
             for q in range(lo, 4):
                 j = 4 * c + q
                 o = vt[:, P * (q - lo) : P * (q - lo + 1)]
@@ -268,9 +284,6 @@ def tile_csocrgattention_kernel(tc, latent, alpha, grad_out, out):
                 klos[t] = klo
                 for c in range(c0):
                     kch[t][c] = klo[:, CH * c : CH * (c + 1)]
-            wrow = work.tile([P, N], F32, tag="w", bufs=2)
-            wrows[t] = wrow
-            wch[t] = [wrow[:, CH * c : CH * (c + 1)] for c in range(NC)]
             tvs[t] = [(c, m if c == c0 else 0) for c in range(c0, NC)]
 
         def n_tk(t):
@@ -301,7 +314,13 @@ def tile_csocrgattention_kernel(tc, latent, alpha, grad_out, out):
                 i = t % NT
                 c0 = i // 4
                 x0 = CEN - P * i
-                nc.gpsimd.tensor_tensor(out=wrows[t][:, CH * c0 : N], in0=kp[i][:], in1=tab[:, x0 + CH * c0 : x0 + N], op=ALU.mult)
+                wrow = work.tile([P, N], F32, tag="w", bufs=2)
+                wrows[t] = wrow
+                wch[t] = [wrow[:, CH * c : CH * (c + 1)] for c in range(NC)]
+                wide = WSPLIT if WSPLIT else N
+                for y in range(CH * c0, N, wide):
+                    z = min(N, y + wide)
+                    nc.gpsimd.tensor_tensor(out=wrows[t][:, y:z], in0=kp[i][:, y - CH * c0 : z - CH * c0], in1=tab[:, x0 + y : x0 + z], op=ALU.mult)
 
         def w_left(t):
             i = t % NT
@@ -352,17 +371,19 @@ def tile_csocrgattention_kernel(tc, latent, alpha, grad_out, out):
 
         def k_phase(t):
             if not live(t):
-                flush_ht(2)
-                flush_ht(3)
                 return
             i = t % NT
             c0, m = divmod(i, 4)
             units = tvs[t]
+            opened = {}
+            for c, lo in units:
+                if EARLYMM and not byvec(t, c):
+                    opened[c] = open_tv(t, (c, lo))
             for idx in range(len(units)):
                 c, lo = units[idx]
-                bank = fill_tv(t, units[idx])
-                if idx < 2:
-                    flush_ht(2 + idx)
+                bank = fill_tv(t, units[idx], opened.get(c))
+                if idx < len(FK):
+                    flush_ht(FK[idx])
                 nw = P * (4 - lo)
                 base = CH * (c - c0)
                 if byvec(t, c):
@@ -380,7 +401,8 @@ def tile_csocrgattention_kernel(tc, latent, alpha, grad_out, out):
                     nc.scalar.activation(
                         out=kp[i][:, 0 : P * lo], in_=bank[:, nw:CH], func=ACT.Copy, accum_out=accds[t][:, 16 + c : 17 + c]
                     )
-            flush_ht(3)
+            for c in FK:
+                flush_ht(c)
 
         def stage_p(t, c):
             b, i = divmod(t, NT)
@@ -401,12 +423,10 @@ def tile_csocrgattention_kernel(tc, latent, alpha, grad_out, out):
 
         def x_phase(t):
             if not live(t):
-                flush_ht(0)
-                flush_ht(1)
                 return
             pbl = [stage_p(t, c) for c in range(NC)]
-            flush_ht(0)
-            flush_ht(1)
+            for c in FX:
+                flush_ht(c)
             one_x(t, 0, pbl[0])
             nc.vector.reciprocal(out=ws[:, t : t + 1], in_=tots[t][:])
             one_x(t, 1, pbl[1])
@@ -414,11 +434,15 @@ def tile_csocrgattention_kernel(tc, latent, alpha, grad_out, out):
             one_x(t, 3, pbl[3])
 
         def h_phase(t, t2):
+            for c in FB:
+                flush_ht(c)
             if live(t):
                 pbl = [stage_p(t, c) for c in range(NC)]
             for c in range(NC):
+                flush_ht(c)
+            for c in range(NC):
                 if live(t):
-                    h = work.tile([P, CH], F32, tag="h", bufs=5)
+                    h = work.tile([P, CH], F32, tag="h", bufs=HB)
                     nc.vector.scalar_tensor_tensor(
                         out=h[:], in0=pbl[c][:], scalar=negcs[t][:, 0:1], in1=wch[t][c], op0=ALU.add, op1=ALU.mult,
                     )
@@ -446,28 +470,41 @@ def tile_csocrgattention_kernel(tc, latent, alpha, grad_out, out):
                     in_=caccs[c][:].rearrange("p (q r) -> p q r", q=4), axis=AX.X, op=ALU.add,
                 )
 
+        turns = TURNS
+        turns[-2] = HEAD
+
         def step(s):
-            if s == NT:
+            if s == NT + DEEP:
                 read_c(0)
             make_until(s + 2)
             make_some(Q0)
+            if QPOS == 0 and s - 1 in turns:
+                g_q(turns[s - 1])
             x_phase(s + 1)
+            if QPOS == 1 and s - 1 in turns:
+                g_q(turns[s - 1])
             small_c(s + 1)
             alloc_step(s + 2)
             k_phase(s + 2)
+            if QPOS == 2 and s - 1 in turns:
+                g_q(turns[s - 1])
             ntk = n_tk(s + 2)
-            w_right(s + 2)
+            w_right(s + 2 - DEEP)
             for c in range(ntk - (1 if (s + 2) % 4 > 0 else 0)):
                 tk_unit(s + 2, c)
-            w_left(s + 2)
+            w_left(s + 2 - DEEP)
             small_s(s + 2)
-            n = HEAD + s + 2
-            if HEAD < n <= len(groups):
-                g_q(n - 1)
-            h_phase(s + 1, s + 2)
-            if HEAD < n + 1 and n < len(groups) and s > -2:
-                g_tr(n, GV)
-                g_load(n + LOADS)
+            if QPOS == 3 and s - 1 in turns:
+                g_q(turns[s - 1])
+            if GPOS == 2 and s in turns and s > -2:
+                g_tr(turns[s], GV)
+                g_load(turns[s] + LOADS)
+            h_phase(s + 1 - DEEP, s + 2)
+            if QPOS == 4 and s - 1 in turns:
+                g_q(turns[s - 1])
+            if GPOS == 0 and s in turns and s > -2:
+                g_tr(turns[s], GV)
+                g_load(turns[s] + LOADS)
 
         g_load(0)
         nc.sync.dma_start(out=abf[0 : B * NT, :], in_=alpha.rearrange("b (t p) -> (b t) p", p=P))
@@ -485,11 +522,10 @@ def tile_csocrgattention_kernel(tc, latent, alpha, grad_out, out):
             if n == HK:
                 step(-2)
         g_q(HEAD - 1)
+        fin = d0
         g_tr(HEAD, GV)
         g_load(HEAD + LOADS)
-        fin = d0
-        nc.vector.memset(fin[:], 0.0)
-        for s in range(-1, STEPS - 1):
+        for s in range(-1, STEPS - 1 + DEEP):
             step(s)
         for c in range(NC):
             flush_ht(c)
@@ -497,6 +533,7 @@ def tile_csocrgattention_kernel(tc, latent, alpha, grad_out, out):
 
         rs = const.tile([P, STEPS], F32)
         nc.vector.tensor_reduce(out=rs[:], in_=rpart[:].rearrange("p (t c) -> p t c", c=NC), axis=AX.X, op=ALU.add)
+        nc.vector.memset(fin[:], 0.0)
         nc.vector.tensor_tensor(out=fin[:, 0:STEPS], in0=rs[:], in1=cs[:], op=ALU.add)
         fps = pst.tile([P, CH], F32, tag="tp")
         nc.tensor.transpose(fps[:, 0:P], fin[:], ident[:])

@@ -37,6 +37,7 @@ EARLYMM = False
 FX, FK, FB = (0, 1), (2, 3), ()
 HB = 8
 GPOS = 2
+PLAIN = 2
 DEEP = 0
 QPOS = 2
 WSPLIT = 0
@@ -300,7 +301,10 @@ def tile_csocrgattention_kernel(tc, latent, alpha, grad_out, out):
             for q in range(nb):
                 j = 4 * c + q
                 off = P * i - CH * c
-                nc.tensor.transpose(kt[:, P * q : P * (q + 1)], kp[j][:, off : off + P], ident[:])
+                if q == 0 and c0 >= PLAIN:
+                    nc.tensor.matmul(out=kt[:, P * q : P * (q + 1)], lhsT=kp[j][:, off : off + P], rhs=ident[:], start=True, stop=True)
+                else:
+                    nc.tensor.transpose(kt[:, P * q : P * (q + 1)], kp[j][:, off : off + P], ident[:])
             dst = kch[t][c] if c < c0 else kp[i][:, 0 : P * m]
             if c < LV[t // NT][c0]:
                 nc.vector.tensor_scalar(

@@ -37,6 +37,7 @@ EARLYMM = False
 FX, FK, FB = (0, 1), (2, 3), ()
 HB = 8
 GPOS = 2
+PLAINH = ((1, 3),)
 PLAIN = 2
 DEEP = 0
 QPOS = 2
@@ -369,7 +370,8 @@ def tile_csocrgattention_kernel(tc, latent, alpha, grad_out, out):
                 caccs[c] = cacc
             for q in range(4):
                 nc.tensor.matmul(
-                    out=caccs[c][:, P * q : P * (q + 1)], lhsT=h[:, P * q : P * (q + 1)], rhs=ident[:], is_transpose=True,
+                    out=caccs[c][:, P * q : P * (q + 1)], lhsT=h[:, P * q : P * (q + 1)], rhs=ident[:],
+                    is_transpose=(c, q) not in PLAINH,
                     start=(i == 0 and q == 0), stop=(i == NT - 1 and q == 3),
                 )
 

from contextlib import ExitStack

import concourse.mybir as mybir
from concourse.masks import make_identity

F32 = mybir.dt.float32
BF16 = mybir.dt.bfloat16
U32 = mybir.dt.uint32
U8 = mybir.dt.uint8
I32 = mybir.dt.int32
E4X4 = mybir.dt.float8_e4m3fn_x4
E5X4 = mybir.dt.float8_e5m2_x4
ACT = mybir.ActivationFunctionType
ALU = mybir.AluOpType
AX = mybir.AxisListType

P = 128
B = 2
N = 2048
D = 512
NT = N // P
CH = 512
NC = N // CH
EPS = 1e-4
LAM = 64.0
CEN = N - P
TABW = 2 * N - P
STEPS = B * NT
LOADS = 3
GV = 1
DG = 6
UL = 8
UR = 4
LEAD = 9
Q0 = 4
EARLYMM = False
FX, FK, FB = (0, 1), (2, 3), ()
HB = 8
GPOS = 2
PLAINH = ((1, 3),)
PLAIN = 2
DEEP = 0
QPOS = 2
WSPLIT = 0
TURNS = {n - 7: n for n in range(6, 16)}
HSPLIT, HK = 3, 4
LV = ((0, 0, 0, 1), (0, 0, 0, 1))
DP = ((0, 0, 0, 0), (0, 0, 0, 0))
NV = ((1, 1, 1, 1), (1, 1, 1, 1))
GC = 0

FLOPS = 2 * B * N * N * D


def tile_csocrgattention_kernel(tc, latent, alpha, grad_out, out):
    nc = tc.nc
    with ExitStack() as ctx:
        const = ctx.enter_context(tc.tile_pool(name="const", bufs=1))
        codes = ctx.enter_context(tc.tile_pool(name="codes", bufs=1))
        stage = ctx.enter_context(tc.tile_pool(name="stage", bufs=2))
        kpool = ctx.enter_context(tc.tile_pool(name="kpool", bufs=1))
        upool = ctx.enter_context(tc.tile_pool(name="upool", bufs=2))
        work = ctx.enter_context(tc.tile_pool(name="work", bufs=3))
        small = ctx.enter_context(tc.tile_pool(name="small", bufs=3))
        pst = ctx.enter_context(tc.psum_pool(name="pst", bufs=5))
        psc = ctx.enter_context(tc.psum_pool(name="psc", bufs=1))
        ctx.enter_context(tc.manual_schedule())

        d0i = const.tile([P, P], I32)
        nc.gpsimd.iota(d0i[:], pattern=[[-1, P]], base=0, channel_multiplier=1)
        rowi = const.tile([P, NT], I32)
        nc.gpsimd.iota(rowi[:], pattern=[[P, NT]], base=-(N // 2), channel_multiplier=1)
        ident = const.tile([P, P], F32)
        make_identity(nc, ident[:])

        d0 = const.tile([P, P], F32)
        nc.vector.tensor_copy(out=d0[:], in_=d0i[:])
        nd0 = const.tile([P, P], F32)
        nc.vector.tensor_scalar(out=nd0[:], in0=d0[:], scalar1=-1.0, scalar2=None, op0=ALU.mult)
        rd = const.tile([P, P], F32)
        nc.vector.tensor_tensor(out=rd[:], in0=d0[:], in1=nd0[:], op=ALU.max)
        ct = const.tile([P, P], F32)
        nc.vector.tensor_scalar(out=ct[:], in0=d0[:], scalar1=0.0, scalar2=2.0 / LAM, op0=ALU.min, op1=ALU.mult)
        br = const.tile([P, NT], F32)
        nc.vector.tensor_scalar(out=br[:], in0=rowi[:], scalar1=1.0 / LAM, scalar2=None, op0=ALU.mult)
        bl = const.tile([P, NT], F32)
        nc.vector.tensor_scalar(out=bl[:], in0=rowi[:], scalar1=-1.0 / LAM, scalar2=-EPS / LAM, op0=ALU.mult, op1=ALU.add)

        tab = const.tile([P, TABW], F32)
        R0 = CEN + P
        for k in range(1, NT):
            nc.scalar.activation(out=tab[:, CEN - P * k : R0 - P * k], in_=d0[:], func=ACT.Ln, bias=P * k + EPS)
        nc.scalar.activation(out=tab[:, CEN:R0], in_=rd[:], func=ACT.Ln, bias=EPS)
        for k in range(1, NT):
            nc.scalar.activation(out=tab[:, CEN + P * k : R0 + P * k], in_=nd0[:], func=ACT.Ln, bias=P * k + EPS)
        sqt = const.tile([P, P], F32)
        nc.scalar.activation(out=sqt[:], in_=rd[:], func=ACT.Exp, scale=-0.5 / LAM, bias=-0.5 * EPS / LAM)

        abf = const.tile([P, P], BF16)
        nc.vector.memset(abf[:], 0.0)
        af = const.tile([P, P], F32)
        nega = const.tile([P, STEPS], F32)

        def make_nega():
            nc.vector.tensor_copy(out=af[:], in_=abf[:])
            aps = pst.tile([P, CH], F32, tag="tp")
            nc.tensor.transpose(aps[:, 0:P], af[:], ident[:])
            nc.vector.tensor_scalar(out=nega[:], in0=aps[:, 0:STEPS], scalar1=-0.5, scalar2=None, op0=ALU.mult)

        ws = const.tile([P, STEPS], F32)
        rpart = const.tile([P, STEPS * NC], F32)
        cs = const.tile([P, STEPS], F32)
        caccs = {}
        junk = const.tile([P, CH], F32)
        sjunk = const.tile([P, 8], F32)

        gc = [codes.tile([P, N], U32, name="gc%d" % b, align_bytes=64) for b in range(B)]
        gs = [codes.tile([P, N], U8, name="gs%d" % b, align_bytes=64) for b in range(B)]
        lc = [codes.tile([P, N], U32, name="lc%d" % b, align_bytes=64) for b in range(B)]
        ls = [codes.tile([P, N], U8, name="ls%d" % b, align_bytes=64) for b in range(B)]

        groups = [(latent, 0, g, lc[0], ls[0], E4X4) for g in range(4)] + [(grad_out, 0, g, gc[0], gs[0], E5X4) for g in range(4)]
        groups += [(latent, 1, g, lc[1], ls[1], E4X4) for g in range(4)] + [(grad_out, 1, g, gc[1], gs[1], E5X4) for g in range(4)]
        HEAD = 5
        xsbs = {}
        grps = {}

        def g_load(n):
            if n < len(groups):
                src, b, g = groups[n][0:3]
                if LOADS <= n < HEAD:
                    xsb = kpool.tile([P, 4, D], BF16, tag="kp%d" % (8 + n - LOADS), name="xh%d" % n)
                else:
                    xsb = stage.tile([P, 4, D], BF16, tag="xsb", bufs=LOADS)
                nc.sync.dma_start(out=xsb[:], in_=src[b, CH * g : CH * (g + 1), :].rearrange("(a p) d -> p a d", p=P))
                xsbs[n] = xsb

        def g_tr(n, on_vector):
            xsb = xsbs[n]
            grp = stage.tile([P, 4 * CH], BF16, tag="grp", align_bytes=64)
            grps[n] = grp
            gview = grp[:].bitcast(F32).rearrange("p (a r u) -> p a r u", a=4, u=2)
            for hf in range(2):
                xt = pst.tile([P, 2, 2, P], F32, tag="tp")
                for a in range(2):
                    words = xsb[:, 2 * hf + a, :].bitcast(F32)
                    for u in range(2):
                        nc.tensor.transpose(xt[:, a, u, :], words[:, P * u : P * (u + 1)], ident[:])
                sview = xt[:].rearrange("p a u r -> p a r u")
                if on_vector > hf:
                    nc.vector.tensor_copy(out=gview[:, 2 * hf : 2 * hf + 2], in_=sview)
                else:
                    nc.scalar.copy(out=gview[:, 2 * hf : 2 * hf + 2], in_=sview)

        def g_q(n):
            g, cod, pla, fmt = groups[n][2:6]
            nc.vector.quantize_mx(
                out=cod[:, CH * g : CH * (g + 1)].bitcast(fmt), scales=pla[:, CH * g : CH * (g + 1)], in_=grps[n][:]
            )

        kp = {}
        urows = {}
        ulcs = {}
        kch = {}
        wch = {}
        accds = {}
        negcs = {}
        tots = {}
        klos = {}
        wrows = {}
        haccs = {}
        tvs = {}

        dgs = {}

        def byvec(t, c):
            b, i = divmod(t, NT)
            d = c - i // 4
            return 0 < d <= NV[b][i // 4] or (d == 0 and not DP[b][i // 4])

        def live(t):
            return 0 <= t < STEPS

        pieces = []
        for t in range(STEPS):
            for c in range((t % NT) // 4, NC):
                pieces.append((t, c, 0))
                if byvec(t, c):
                    pieces.append((t, c, 1))
        made = [0]
        used = [0]

        def make_u():
            if made[0] == len(pieces):
                return False
            t, c, half = pieces[made[0]]
            b, i = divmod(t, NT)
            if half == 0:
                if not byvec(t, c) and t not in dgs:
                    dg = upool.tile([P, P], F32, tag="dg", bufs=DG)
                    nc.scalar.activation(out=dg[:], in_=ident[:], func=ACT.Copy, scale=nega[:, t : t + 1])
                    dgs[t] = dg
                ulc = upool.tile([P, CH], F32, tag="ulc", bufs=UL)
                for j in range(max(i + byvec(t, c), 4 * c), 4 * c + 4):
                    blk = NT - 1 - j + i
                    nc.scalar.activation(
                        out=ulc[:, P * (j - 4 * c) : P * (j - 4 * c + 1)], in_=tab[:, P * blk : P * (blk + 1)],
                        func=ACT.Exp if byvec(t, c) else ACT.Identity,
                        scale=nega[:, b * NT + j : b * NT + j + 1], bias=bl[:, j : j + 1],
                    )
                ulcs[(t, c)] = ulc
            else:
                urow = upool.tile([P, CH], F32, tag="urow", bufs=UR)
                x0 = CEN - P * i + CH * c
                lo = 0
                if c == i // 4:
                    lo = i % 4 + 1
                    ud0 = upool.tile([P, P], F32, tag="ud0", bufs=2)
                    nc.scalar.activation(out=ud0[:], in_=tab[:, CEN:R0], func=ACT.Exp, scale=nega[:, t : t + 1])
                    nc.gpsimd.tensor_tensor(out=urow[:, P * (lo - 1) : P * lo], in0=ud0[:], in1=sqt[:], op=ALU.mult)
                if lo < 4:
                    nc.scalar.activation(
                        out=urow[:, P * lo : CH], in_=tab[:, x0 + P * lo : x0 + CH], func=ACT.Exp,
                        scale=nega[:, t : t + 1], bias=br[:, i : i + 1],
                    )
                urows[(t, c)] = urow
            made[0] += 1
            return True

        def can_make():
            return made[0] < len(pieces) and made[0] - used[0] < LEAD

        def make_some(n):
            for q in range(n):
                if can_make():
                    make_u()

        def make_until(t):
            while made[0] < len(pieces) and pieces[made[0]][0] <= t:
                make_u()

        def open_tv(t, unit):
            i = t % NT
            c, lo = unit
            nw = P * (4 - lo)
            x0 = CEN - P * i + CH * c + P * lo
            vt = pst.tile([P, CH], F32, tag="tp")
            nc.tensor.matmul(out=vt[:, 0:nw], lhsT=dgs[t][:], rhs=tab[:, x0 : x0 + nw], start=True, stop=False)
            return vt

        def fill_tv(t, unit, vt=None):
            i = t % NT
            c, lo = unit
            if vt is None and byvec(t, c):
                vt = pst.tile([P, CH], F32, tag="tp")
            elif vt is None:
                vt = open_tv(t, unit)
            used[0] += 2 if byvec(t, c) else 1
            for q in range(lo, 4):
                j = 4 * c + q
                o = vt[:, P * (q - lo) : P * (q - lo + 1)]
                if byvec(t, c):
                    srcb = urows[(t, c)][:, P * q : P * (q + 1)] if j == i else ulcs[(t, c)][:, P * q : P * (q + 1)]
                    nc.tensor.transpose(o, srcb, ident[:])
                else:
                    srcb = ulcs[(t, c)][:, P * q : P * (q + 1)]
                    nc.tensor.matmul(out=o, lhsT=srcb, rhs=ident[:], is_transpose=True, start=False, stop=(q == 3 and j != i))
                    if j == i:
                        nc.tensor.matmul(out=o, lhsT=ct[:], rhs=ident[:], is_transpose=True, start=False, stop=(q == 3))
            for q in range(lo):
                nc.tensor.transpose(vt[:, P * (4 - lo + q) : P * (5 - lo + q)], kp[4 * c + q][:, P * i - CH * c : P * (i + 1) - CH * c], ident[:])
            return vt

        def alloc_step(t):
            if not live(t):
                return
            b, i = divmod(t, NT)
            c0, m = divmod(i, 4)
            kpi = kpool.tile([P, N - CH * c0], F32, tag="kp%d" % i, name="kp%d_%d" % (i, b))
            kp[i] = kpi
            accd = small.tile([P, 24], F32, tag="accd")
            accds[t] = accd
            kch[t] = [None] * c0 + [kpi[:, CH * (c - c0) : CH * (c - c0 + 1)] for c in range(c0, NC)]
            if c0 > 0:
                klo = work.tile([P, CH * (NC - 1)], F32, tag="klo", bufs=2)
                klos[t] = klo
                for c in range(c0):
                    kch[t][c] = klo[:, CH * c : CH * (c + 1)]
            tvs[t] = [(c, m if c == c0 else 0) for c in range(c0, NC)]

        def n_tk(t):
            if not live(t):
                return 0
            c0, m = divmod(t % NT, 4)
            return c0 + (1 if m > 0 else 0)

        def tk_unit(t, c):
            i = t % NT
            c0, m = divmod(i, 4)
            nb = 4 if c < c0 else m
            kt = pst.tile([P, CH], F32, tag="tp")
            for q in range(nb):
                j = 4 * c + q
                off = P * i - CH * c
                if q == 0 and c0 >= PLAIN:
                    nc.tensor.matmul(out=kt[:, P * q : P * (q + 1)], lhsT=kp[j][:, off : off + P], rhs=ident[:], start=True, stop=True)
                else:
                    nc.tensor.transpose(kt[:, P * q : P * (q + 1)], kp[j][:, off : off + P], ident[:])
            dst = kch[t][c] if c < c0 else kp[i][:, 0 : P * m]
            if c < LV[t // NT][c0]:
                nc.vector.tensor_scalar(
                    out=dst, in0=kt[:], scalar1=1.0, scalar2=None, op0=ALU.mult, op1=ALU.add, accum_out=accds[t][:, 16 + c : 17 + c]
                )
            else:
                nc.scalar.activation(out=dst, in_=kt[:, 0 : P * nb], func=ACT.Copy, accum_out=accds[t][:, 16 + c : 17 + c])

        def w_right(t):
            if live(t):
                i = t % NT
                c0 = i // 4
                x0 = CEN - P * i
                wrow = work.tile([P, N], F32, tag="w", bufs=2)
                wrows[t] = wrow
                wch[t] = [wrow[:, CH * c : CH * (c + 1)] for c in range(NC)]
                wide = WSPLIT if WSPLIT else N
                for y in range(CH * c0, N, wide):
                    z = min(N, y + wide)
                    nc.gpsimd.tensor_tensor(out=wrows[t][:, y:z], in0=kp[i][:, y - CH * c0 : z - CH * c0], in1=tab[:, x0 + y : x0 + z], op=ALU.mult)

        def w_left(t):
            i = t % NT
            c0 = i // 4
            n = CH * c0
            if live(t) and n > 0:
                x0 = CEN - P * i
                nc.gpsimd.tensor_tensor(out=wrows[t][:, 0:n], in0=klos[t][:, 0:n], in1=tab[:, x0 : x0 + n], op=ALU.mult)

        def small_s(t):
            if live(t):
                c0, m = divmod(t % NT, 4)
                na = c0 + (1 if m > 0 else 0)
                n = NC - c0 + na
                tot = small.tile([P, 1], F32, tag="tot")
                nc.scalar.activation(
                    out=sjunk[:, 0:n], in_=accds[t][:, 12 + c0 : 16 + na], func=ACT.Copy, scale=-1.0, bias=-1e-8 / n,
                    accum_out=tot[:],
                )
                tots[t] = tot

        def small_c(t):
            if live(t):
                negc = small.tile([P, 1], F32, tag="negc")
                nc.scalar.activation(
                    out=sjunk[:, 0:NC], in_=accds[t][:, 0:NC], func=ACT.Copy, scale=ws[:, t : t + 1], accum_out=negc[:],
                )
                negcs[t] = negc

        pending = {}

        def flush_ht(c):
            if pending.get(c) is None:
                return
            t, h = pending[c]
            pending[c] = None
            if c == GC:
                return
            i = t % NT
            if i == 0:
                cacc = psc.tile([P, CH], F32, tag="ca%d" % c, name="ca%d_%d" % (c, t))
                caccs[c] = cacc
            for q in range(4):
                nc.tensor.matmul(
                    out=caccs[c][:, P * q : P * (q + 1)], lhsT=h[:, P * q : P * (q + 1)], rhs=ident[:],
                    is_transpose=(c, q) not in PLAINH,
                    start=(i == 0 and q == 0), stop=(i == NT - 1 and q == 3),
                )

        def k_phase(t):
            if not live(t):
                return
            i = t % NT
            c0, m = divmod(i, 4)
            units = tvs[t]
            opened = {}
            for c, lo in units:
                if EARLYMM and not byvec(t, c):
                    opened[c] = open_tv(t, (c, lo))
            for idx in range(len(units)):
                c, lo = units[idx]
                bank = fill_tv(t, units[idx], opened.get(c))
                if idx < len(FK):
                    flush_ht(FK[idx])
                nw = P * (4 - lo)
                base = CH * (c - c0)
                if byvec(t, c):
                    nc.vector.scalar_tensor_tensor(
                        out=kp[i][:, base + P * lo : base + CH], in0=bank[:, 0:nw], scalar=1.0,
                        in1=urows[(t, c)][:, P * lo : CH], op0=ALU.mult, op1=ALU.mult,
                        accum_out=accds[t][:, 12 + c : 13 + c],
                    )
                else:
                    nc.scalar.activation(
                        out=kp[i][:, base + P * lo : base + CH], in_=bank[:, 0:nw], func=ACT.Exp, bias=br[:, i : i + 1],
                        accum_out=accds[t][:, 12 + c : 13 + c],
                    )
                if lo > 0:
                    nc.scalar.activation(
                        out=kp[i][:, 0 : P * lo], in_=bank[:, nw:CH], func=ACT.Copy, accum_out=accds[t][:, 16 + c : 17 + c]
                    )
            for c in FK:
                flush_ht(c)

        def stage_p(t, c):
            b, i = divmod(t, NT)
            pb = pst.tile([P, CH], F32, tag="tp")
            nc.tensor.matmul_mx(
                out=pb[:],
                lhsT=gc[b][:, P * i : P * (i + 1)].bitcast(E5X4), lhsT_scale=gs[b][:, P * i : P * (i + 1)],
                rhs=lc[b][:, CH * c : CH * (c + 1)].bitcast(E4X4), rhs_scale=ls[b][:, CH * c : CH * (c + 1)],
                start=True, stop=True,
            )
            return pb

        def one_x(t, c, pb):
            nc.vector.scalar_tensor_tensor(
                out=junk[:], in0=pb[:], scalar=1.0, in1=kch[t][c], op0=ALU.mult, op1=ALU.mult,
                accum_out=accds[t][:, c : c + 1],
            )

        def x_phase(t):
            if not live(t):
                return
            pbl = [stage_p(t, c) for c in range(NC)]
            for c in FX:
                flush_ht(c)
            one_x(t, 0, pbl[0])
            nc.vector.reciprocal(out=ws[:, t : t + 1], in_=tots[t][:])
            one_x(t, 1, pbl[1])
            one_x(t, 2, pbl[2])
            one_x(t, 3, pbl[3])

        def h_phase(t, t2):
            for c in FB:
                flush_ht(c)
            if live(t):
                pbl = [stage_p(t, c) for c in range(NC)]
            for c in range(NC):
                flush_ht(c)
            for c in range(NC):
                if live(t):
                    h = work.tile([P, CH], F32, tag="h", bufs=HB)
                    nc.vector.scalar_tensor_tensor(
                        out=h[:], in0=pbl[c][:], scalar=negcs[t][:, 0:1], in1=wch[t][c], op0=ALU.add, op1=ALU.mult,
                    )
                    first = c == GC and t % NT == 0
                    if first:
                        hacc = work.tile([P, CH], F32, tag="hacc", bufs=2)
                        haccs[t // NT] = hacc
                    nc.scalar.activation(
                        out=haccs[t // NT][:] if first else h[:], in_=h[:], func=ACT.Copy, scale=ws[:, t : t + 1],
                        accum_out=rpart[:, NC * t + c : NC * t + c + 1],
                    )
                    pending[c] = (t, h)
            if live(t) and t % NT > 0:
                hacc = haccs[t // NT]
                nc.gpsimd.tensor_tensor(out=hacc[:], in0=hacc[:], in1=pending[GC][1][:], op=ALU.add)

        def read_c(b):
            gt = pst.tile([P, CH], F32, tag="tp")
            for q in range(4):
                nc.tensor.transpose(gt[:, P * q : P * (q + 1)], haccs[b][:, P * q : P * (q + 1)], ident[:])
            caccs[GC] = gt
            for c in [c for c in range(NC) if c != GC] + [GC]:
                nc.vector.tensor_reduce(
                    out=cs[:, NT * b + 4 * c : NT * b + 4 * (c + 1)],
                    in_=caccs[c][:].rearrange("p (q r) -> p q r", q=4), axis=AX.X, op=ALU.add,
                )

        turns = TURNS
        turns[-2] = HEAD

        def step(s):
            if s == NT + DEEP:
                read_c(0)
            make_until(s + 2)
            make_some(Q0)
            if QPOS == 0 and s - 1 in turns:
                g_q(turns[s - 1])
            x_phase(s + 1)
            if QPOS == 1 and s - 1 in turns:
                g_q(turns[s - 1])
            small_c(s + 1)
            alloc_step(s + 2)
            k_phase(s + 2)
            if QPOS == 2 and s - 1 in turns:
                g_q(turns[s - 1])
            ntk = n_tk(s + 2)
            w_right(s + 2 - DEEP)
            for c in range(ntk - (1 if (s + 2) % 4 > 0 else 0)):
                tk_unit(s + 2, c)
            w_left(s + 2 - DEEP)
            small_s(s + 2)
            if QPOS == 3 and s - 1 in turns:
                g_q(turns[s - 1])
            if GPOS == 2 and s in turns and s > -2:
                g_tr(turns[s], GV)
                g_load(turns[s] + LOADS)
            h_phase(s + 1 - DEEP, s + 2)
            if QPOS == 4 and s - 1 in turns:
                g_q(turns[s - 1])
            if GPOS == 0 and s in turns and s > -2:
                g_tr(turns[s], GV)
                g_load(turns[s] + LOADS)

        g_load(0)
        nc.sync.dma_start(out=abf[0 : B * NT, :], in_=alpha.rearrange("b (t p) -> (b t) p", p=P))
        for n in range(1, HEAD):
            g_load(n)
        for n in range(HEAD):
            g_tr(n, 2 if n < HSPLIT else 1)
            if n < LOADS:
                g_load(n + HEAD)
            if n == 0:
                make_nega()
                make_until(0)
            if n > 0:
                g_q(n - 1)
            if n == HK:
                step(-2)
        g_q(HEAD - 1)
        fin = d0
        g_tr(HEAD, GV)
        g_load(HEAD + LOADS)
        for s in range(-1, STEPS - 1 + DEEP):
            step(s)
        for c in range(NC):
            flush_ht(c)
        read_c(1)

        rs = const.tile([P, STEPS], F32)
        nc.vector.tensor_reduce(out=rs[:], in_=rpart[:].rearrange("p (t c) -> p t c", c=NC), axis=AX.X, op=ALU.add)
        nc.vector.memset(fin[:], 0.0)
        nc.vector.tensor_tensor(out=fin[:, 0:STEPS], in0=rs[:], in1=cs[:], op=ALU.add)
        fps = pst.tile([P, CH], F32, tag="tp")
        nc.tensor.transpose(fps[:, 0:P], fin[:], ident[:])
        osb = nd0
        nc.vector.tensor_scalar(out=osb[:], in0=fps[:, 0:P], scalar1=0.5, scalar2=None, op0=ALU.mult)
        nc.sync.dma_start(out=out.rearrange("b (t p) -> (b t) p", p=P), in_=osb[0:STEPS, :])
